import numpy as np
import ml_dtypes


def mxq(x, axis, fmt="e4m3"):
    dtype, down = {"e4m3": (ml_dtypes.float8_e4m3fn, 7), "e5m2": (ml_dtypes.float8_e5m2, 14)}[fmt]
    v = np.moveaxis(np.asarray(x, np.float32).astype(ml_dtypes.bfloat16).astype(np.float64), axis, -1)
    blocks = v.reshape(v.shape[:-1] + (-1, 32))
    amax = np.abs(blocks).max(-1, keepdims=True)
    byte = np.maximum(np.where(amax > 0, np.frexp(amax)[1] - 1 + 127, 0) - down, 1)
    scale = np.exp2(byte - 127.0)
    codes = (blocks / scale).astype(np.float32).astype(dtype).astype(np.float64)
    return np.moveaxis((codes * scale).reshape(v.shape), -1, axis)


WIDE = False


def mx_kscale(k):
    if not WIDE:
        return np.ones(k)
    levels = np.array([10, -10, 5, -5, 0])
    a = np.random.permutation(np.resize(levels, k // 512 * 4)).reshape(k // 512, 4)
    idx = np.arange(k)
    return np.exp2(a[idx // 512, idx % 128 // 32])


BF16 = ml_dtypes.bfloat16


def bf(x):
    return np.asarray(x, np.float32).astype(BF16)


def f64(x):
    return np.asarray(x).astype(np.float64)


E2M1 = np.array([0.0, 0.5, 1.0, 1.5, 2.0, 3.0, 4.0, 6.0, -0.0, -0.5, -1.0, -1.5, -2.0, -3.0, -4.0, -6.0])


def pack_weight(w, fmt):
    k, n = w.shape
    w = f64(bf(w)).reshape(k // 32, 32, n)
    amax = np.abs(w).max(1)
    if fmt == "e4m3":
        byte = np.frexp(amax)[1] - 1 + 127 - 7
    else:
        mant, ex = np.frexp(amax / 6.0)
        byte = np.where(mant > 0.5, ex, ex - 1) + 127
    byte = np.clip(np.where(amax > 0, byte, 1), 1, 254)
    scaled = (w * np.exp2(127.0 - byte)[:, None, :]).reshape(k, n).astype(np.float32)
    by_word = np.ascontiguousarray(scaled.reshape(k // 512, 128, 4, n).transpose(0, 1, 3, 2))
    if fmt == "e4m3":
        words = by_word.astype(ml_dtypes.float8_e4m3fn).view(np.uint8)
    else:
        c = by_word.astype(ml_dtypes.float4_e2m1fn).view(np.uint8) & 0xF
        words = c[..., 0::2] | (c[..., 1::2] << 4)
    return np.ascontiguousarray(words), np.ascontiguousarray(byte.astype(np.uint8).reshape(k // 512, 16, n))


def unpack_weight(words, scales, fmt):
    g, p, n, _ = words.shape
    if fmt == "e4m3":
        vals = np.ascontiguousarray(words).view(ml_dtypes.float8_e4m3fn).astype(np.float64)
    else:
        nib = np.empty((g, p, n, 4), np.uint8)
        nib[..., 0::2] = words & 0xF
        nib[..., 1::2] = words >> 4
        vals = E2M1[nib]
    vals = vals * np.repeat(np.exp2(scales.astype(np.float64) - 127.0), 8, axis=1)[..., None]
    return vals.transpose(0, 1, 3, 2).reshape(g * 512, n)


B, M, N, P = 2, 512, 16384, 256
EPS = 1e-05
FMT = "e4m3"


def normalize(v, axes, gamma, beta):
    mean = v.mean(axis=axes, keepdims=True)
    std = np.sqrt(v.var(axis=axes, keepdims=True, ddof=1))
    return gamma * ((v - mean) / (std + EPS)) + beta


def setup_inputs():
    s = mx_kscale(N)
    x = bf(np.random.standard_normal((B, M, N)) * s)
    xj_words, xj_scales = pack_weight(np.random.standard_normal((N, P)) * 0.5 / np.sqrt(N) / s[:, None], FMT)
    xi_words, xi_scales = pack_weight(np.random.standard_normal((M, P)) * 2.0 / np.sqrt(M), FMT)
    return {"x": x,
            "original_xj_y_words": xj_words,
            "original_xj_y_scales": xj_scales,
            "original_xi_y_words": xi_words,
            "original_xi_y_scales": xi_scales,
            "gamma_o_sum": bf(1.0 + 0.1 * np.random.standard_normal(P)),
            "gamma_o": bf(1.0 + 0.1 * np.random.standard_normal((P, P))),
            "beta_o_sum": bf(0.1 * np.random.standard_normal(P)),
            "beta_o": bf(0.1 * np.random.standard_normal((P, P)))}


def reference(x, original_xj_y_words, original_xj_y_scales, original_xi_y_words, original_xi_y_scales, gamma_o_sum, gamma_o, beta_o_sum, beta_o):
    oyy = mxq(f64(x), 2, "e4m3") @ unpack_weight(original_xj_y_words, original_xj_y_scales, FMT)
    o_sum = normalize(oyy.sum(axis=-2), (-1,), f64(gamma_o_sum), f64(beta_o_sum)) + 1.0
    oyy = mxq(np.swapaxes(oyy, -1, -2), 2, "e4m3") @ unpack_weight(original_xi_y_words, original_xi_y_scales, FMT)
    oyy = np.swapaxes(oyy, -1, -2)
    oyy = normalize(oyy, (-2, -1), f64(gamma_o), f64(beta_o))
    return oyy, o_sum

@@ -1,0 +1,303 @@
+from contextlib import ExitStack
+
+import concourse.mybir as mybir
+from concourse.masks import make_identity
+
+BF16 = mybir.dt.bfloat16
+F32 = mybir.dt.float32
+I32 = mybir.dt.int32
+U32 = mybir.dt.uint32
+U8 = mybir.dt.uint8
+FP8X4 = mybir.dt.float8_e4m3fn_x4
+ALU = mybir.AluOpType
+ACT = mybir.ActivationFunctionType
+
+P = 128
+PACK = 4
+K_PASS = P * PACK
+BATCH, M, K, N = 2, 512, 16384, 256
+EPS = 1e-05
+
+PASSES = K // K_PASS
+ROW_TILES = M // P
+HALVES = N // P
+WORDS = K_PASS // 2
+RUN_PASSES = 2
+RUN_K = RUN_PASSES * K_PASS
+CHUNKS = PASSES // RUN_PASSES
+RUNS = CHUNKS * BATCH
+BANK_COLS = 256
+X_BUFS = 8
+
+FLOPS = 2 * BATCH * M * K * N + 2 * BATCH * N * M * N
+
+
+def tile_selfprojection_pa_k_kernel(
+    tc,
+    x,
+    original_xj_y_words,
+    original_xj_y_scales,
+    original_xi_y_words,
+    original_xi_y_scales,
+    gamma_o_sum,
+    gamma_o,
+    beta_o_sum,
+    beta_o,
+    out_0,
+    out_1,
+):
+    nc = tc.nc
+    with ExitStack() as ctx:
+        const = ctx.enter_context(tc.tile_pool(name="const", bufs=1))
+        x_pool = ctx.enter_context(tc.tile_pool(name="x_pool", bufs=X_BUFS))
+        w_pool = ctx.enter_context(tc.tile_pool(name="w_pool", bufs=CHUNKS))
+        work = ctx.enter_context(tc.tile_pool(name="work", bufs=3))
+        tail = ctx.enter_context(tc.tile_pool(name="tail", bufs=1))
+        sums = ctx.enter_context(tc.psum_pool(name="sums", bufs=1))
+        banks = ctx.enter_context(tc.psum_pool(name="banks", bufs=4))
+
+        wj_scales = const.tile([P, PASSES, N], U8, align_bytes=64)
+        nc.vector.memset(wj_scales[:].bitcast(I32), 0)
+        wi_scales = const.tile([P, N], U8, align_bytes=64)
+        nc.vector.memset(wi_scales[:].bitcast(I32), 0)
+
+        ident = const.tile([P, P], F32)
+        make_identity(nc, ident[:])
+        averager = const.tile([P, P], F32)
+        nc.vector.memset(averager[:], 1.0 / P)
+        warm = const.tile([P, 1], F32)
+        nc.vector.memset(warm[:], 1.0)
+        nc.scalar.sqrt(out=warm[:], in_=warm[:])
+
+        wj_words = original_xj_y_words.rearrange("g p n t -> g p (n t)").bitcast(I32)
+        x_tiles = {}
+        w_tiles = {}
+        sorted_tiles = {}
+        grouped_tiles = {}
+        code_tiles = {}
+
+        y_t_sums = {}
+        for b in range(BATCH):
+            for h in range(HALVES):
+                y_t_sums[b, h] = sums.tile([P, M], F32, name="sum%d%d" % (b, h))
+
+        def load(run):
+            chunk, b = divmod(run, BATCH)
+            xs = x_pool.tile([P, ROW_TILES, RUN_K], BF16)
+            nc.sync.dma_start(
+                out=xs[:],
+                in_=x[b, :, chunk * RUN_K : (chunk + 1) * RUN_K].rearrange("(r t) k -> r t k", t=ROW_TILES),
+            )
+            x_tiles[run] = xs
+            if b == 0:
+                wj = w_pool.tile([P, RUN_PASSES, N], U32, align_bytes=64)
+                nc.sync.dma_start(
+                    out=wj[:].bitcast(I32),
+                    in_=wj_words[chunk * RUN_PASSES : (chunk + 1) * RUN_PASSES].rearrange("g p n -> p g n"),
+                )
+                w_tiles[chunk] = wj
+
+        def sort_words(run):
+            xs_words = x_tiles[run][:].bitcast(F32)
+            planes = work.tile([P, RUN_PASSES, ROW_TILES, 2, P], F32)
+            for g in range(RUN_PASSES):
+                nc.vector.tensor_copy(
+                    out=planes[:, g],
+                    in_=xs_words[:, :, g * WORDS : (g + 1) * WORDS].rearrange("r t (j u) -> r t u j", u=2),
+                )
+            sorted_tiles[run] = planes
+
+        def transpose(run):
+            planes = sorted_tiles[run]
+            grouped = work.tile([P, RUN_PASSES, M, PACK], BF16, align_bytes=64)
+            grouped_words = grouped[:].bitcast(F32)
+            for g in range(RUN_PASSES):
+                for c in range(M // BANK_COLS):
+                    bank = banks.tile([P, 2, BANK_COLS], F32)
+                    for i in range(BANK_COLS // P):
+                        for u in range(2):
+                            nc.tensor.transpose(
+                                out=bank[:, u, i * P : (i + 1) * P],
+                                in_=planes[:, g, c * (BANK_COLS // P) + i, u, :],
+                                identity=ident[:],
+                            )
+                    nc.scalar.copy(
+                        out=grouped_words[:, g, c * BANK_COLS : (c + 1) * BANK_COLS, :],
+                        in_=bank[:].rearrange("p u m -> p m u"),
+                    )
+            grouped_tiles[run] = grouped
+
+        def quantise(run):
+            grouped = grouped_tiles[run]
+            codes = work.tile([P, RUN_PASSES, M], U32, align_bytes=64)
+            scales = work.tile([P, RUN_PASSES, M], U8, align_bytes=64)
+            for g in range(RUN_PASSES):
+                nc.vector.quantize_mx(
+                    out=codes[:, g, :].bitcast(FP8X4),
+                    scales=scales[:, g, :],
+                    in_=grouped[:, g].rearrange("p m t -> p (m t)"),
+                )
+            code_tiles[run] = (codes, scales)
+
+        def multiply(run):
+            chunk, b = divmod(run, BATCH)
+            codes, scales = code_tiles[run]
+            for g in range(RUN_PASSES):
+                k_pass = chunk * RUN_PASSES + g
+                for h in range(HALVES):
+                    nc.tensor.matmul_mx(
+                        out=y_t_sums[b, h][:],
+                        lhsT=w_tiles[chunk][:, g, h * P : (h + 1) * P].bitcast(FP8X4),
+                        lhsT_scale=wj_scales[:, k_pass, h * P : (h + 1) * P],
+                        rhs=codes[:, g, :].bitcast(FP8X4),
+                        rhs_scale=scales[:, g, :],
+                        start=(k_pass == 0),
+                        stop=(k_pass == PASSES - 1),
+                    )
+
+        with tc.manual_schedule():
+            load(0)
+            wj_scale_rows = original_xj_y_scales.bitcast(I32).rearrange("g (q r) n -> r q g n", r=4)
+            for r in range(4):
+                nc.sync.dma_start(out=wj_scales[r:P:32].bitcast(I32), in_=wj_scale_rows[r])
+            for step in range(RUNS + 3):
+                if step + 1 < RUNS:
+                    load(step + 1)
+                if step < RUNS:
+                    sort_words(step)
+                if 0 <= step - 1 < RUNS:
+                    transpose(step - 1)
+                if 0 <= step - 2 < RUNS:
+                    quantise(step - 2)
+                if 0 <= step - 3 < RUNS:
+                    multiply(step - 3)
+
+            wi = const.tile([P, N], U32, align_bytes=64)
+            nc.sync.dma_start(
+                out=wi[:].bitcast(I32),
+                in_=original_xi_y_words.rearrange("g p n t -> (g p) (n t)").bitcast(I32),
+            )
+            wi_scale_rows = original_xi_y_scales.bitcast(I32).rearrange("g (q r) n -> r (g q) n", r=4)
+            for r in range(4):
+                nc.sync.dma_start(out=wi_scales[r:P:32].bitcast(I32), in_=wi_scale_rows[r])
+            gain = const.tile([P, HALVES, N], BF16)
+            nc.sync.dma_start(out=gain[:], in_=gamma_o.rearrange("(h i) j -> i h j", h=HALVES))
+            bias = const.tile([P, HALVES, N], BF16)
+            nc.sync.dma_start(out=bias[:], in_=beta_o.rearrange("(h i) j -> i h j", h=HALVES))
+            gain_row = const.tile([1, N], BF16)
+            nc.sync.dma_start(out=gain_row[:], in_=gamma_o_sum.rearrange("(o j) -> o j", o=1))
+            bias_row = const.tile([1, N], BF16)
+            nc.sync.dma_start(out=bias_row[:], in_=beta_o_sum.rearrange("(o j) -> o j", o=1))
+
+        bias_row_plus_1 = const.tile([1, N], F32)
+        nc.vector.tensor_scalar_add(out=bias_row_plus_1[:], in0=bias_row[:], scalar1=1.0)
+        o_sum_rows = const.tile([1, BATCH, N], F32)
+
+        def one_over_spread(variance, count, label):
+            spread = tail.tile([P, 1], F32, name="spread_" + label)
+            nc.scalar.activation(out=spread[:], in_=variance, func=ACT.Sqrt, scale=count / (count - 1.0))
+            nc.vector.tensor_scalar_add(out=spread[:], in0=spread[:], scalar1=EPS)
+            inverse = tail.tile([P, 1], F32, name="inverse_" + label)
+            nc.vector.reciprocal(out=inverse[:], in_=spread[:])
+            return inverse
+
+        for b in range(BATCH):
+            y_t = tail.tile([P, HALVES, M], F32, name="y_t%d" % b)
+            c_cols = []
+            for h in range(HALVES):
+                c_col = tail.tile([P, 1], F32, name="c_col%d%d" % (b, h))
+                nc.scalar.activation(out=y_t[:, h, :], in_=y_t_sums[b, h][:], func=ACT.Copy, accum_out=c_col[:])
+                c_cols.append(c_col)
+
+            y_grouped = tail.tile([P, N, PACK], BF16, name="y_grouped%d" % b, align_bytes=64)
+            for h in range(HALVES):
+                y_bank = banks.tile([P, PACK, P], F32, tag="bank", name="y_bank%d%d" % (b, h))
+                for t in range(PACK):
+                    nc.tensor.transpose(out=y_bank[:, t, :], in_=y_t[:, h, t * P : (t + 1) * P], identity=ident[:])
+                copy_out = nc.scalar.copy if h == 0 else nc.vector.tensor_copy
+                copy_out(out=y_grouped[:, h * P : (h + 1) * P, :], in_=y_bank[:].rearrange("r t j -> r j t"))
+            y_codes = tail.tile([P, N], U32, name="y_codes%d" % b, align_bytes=64)
+            y_scales = tail.tile([P, N], U8, name="y_scales%d" % b, align_bytes=64)
+            nc.vector.quantize_mx(
+                out=y_codes[:].bitcast(FP8X4),
+                scales=y_scales[:],
+                in_=y_grouped[:].rearrange("r j t -> r (j t)"),
+            )
+            z = sums.tile([P, HALVES, N], F32, tag="sum%d0" % b, name="z%d" % b)
+            for h in range(HALVES):
+                nc.tensor.matmul_mx(
+                    out=z[:, h, :],
+                    lhsT=wi[:, h * P : (h + 1) * P].bitcast(FP8X4),
+                    lhsT_scale=wi_scales[:, h * P : (h + 1) * P],
+                    rhs=y_codes[:].bitcast(FP8X4),
+                    rhs_scale=y_scales[:],
+                    start=True,
+                    stop=True,
+                )
+
+            z_flat = z[:].rearrange("i h j -> i (h j)")
+            z_stats = tail.tile([P, 6], F32, name="z_stats%d" % b)
+            nc.vector.bn_stats(out=z_stats[:], in_=z_flat)
+            z_mv = tail.tile([P, 2], F32, name="z_mv%d" % b)
+            nc.vector.bn_aggr(out=z_mv[:], in_=z_stats[:])
+            over_all = sums.tile([P, 2], F32, tag="sum%d1" % b, name="over_all%d" % b)
+            nc.tensor.matmul(out=over_all[:, 0:1], lhsT=averager[:], rhs=z_mv[:, 0:1], start=True, stop=True)
+            z_mean = tail.tile([P, 1], F32, name="z_mean%d" % b)
+            nc.vector.tensor_copy(out=z_mean[:], in_=over_all[:, 0:1])
+            distance = tail.tile([P, 1], F32, name="distance%d" % b)
+            nc.vector.tensor_sub(out=distance[:], in0=z_mv[:, 0:1], in1=z_mean[:])
+            part_var = tail.tile([P, 1], F32, name="part_var%d" % b)
+            nc.vector.scalar_tensor_tensor(
+                out=part_var[:], in0=distance[:], scalar=distance[:], in1=z_mv[:, 1:2], op0=ALU.mult, op1=ALU.add
+            )
+            nc.tensor.matmul(out=over_all[:, 1:2], lhsT=averager[:], rhs=part_var[:], start=True, stop=True)
+            centred = tail.tile([P, HALVES * N], F32, name="centred%d" % b)
+            nc.vector.scalar_tensor_tensor(
+                out=centred[:],
+                in0=z_flat,
+                scalar=z_mean[:],
+                in1=gain[:].rearrange("i h j -> i (h j)"),
+                op0=ALU.subtract,
+                op1=ALU.mult,
+            )
+            z_inverse = one_over_spread(over_all[:, 1:2], float(N * N), "z%d" % b)
+            result = tail.tile([P, HALVES, N], F32, name="result%d" % b)
+            nc.vector.scalar_tensor_tensor(
+                out=result[:].rearrange("i h j -> i (h j)"),
+                in0=centred[:],
+                scalar=z_inverse[:],
+                in1=bias[:].rearrange("i h j -> i (h j)"),
+                op0=ALU.mult,
+                op1=ALU.add,
+            )
+            nc.sync.dma_start(out=out_0[b].rearrange("(h i) j -> i h j", h=HALVES), in_=result[:])
+
+            c_rows = banks.tile([P, N], F32, tag="bank", name="c_rows%d" % b)
+            for h in range(HALVES):
+                nc.tensor.matmul(
+                    out=c_rows[:, h * P : (h + 1) * P],
+                    lhsT=c_cols[h][:].to_broadcast([P, P]),
+                    rhs=ident[:],
+                    start=True,
+                    stop=True,
+                )
+            c_stats = tail.tile([P, 6], F32, name="c_stats%d" % b)
+            nc.vector.bn_stats(out=c_stats[:], in_=c_rows[:])
+            c_mv = tail.tile([P, 2], F32, name="c_mv%d" % b)
+            nc.vector.bn_aggr(out=c_mv[:], in_=c_stats[:])
+            c_inverse = one_over_spread(c_mv[:, 1:2], float(N), "c%d" % b)
+            c_centred = tail.tile([1, N], F32, name="c_centred%d" % b)
+            nc.vector.scalar_tensor_tensor(
+                out=c_centred[:], in0=c_rows[0:1, :], scalar=c_mv[0:1, 0:1], in1=gain_row[:], op0=ALU.subtract, op1=ALU.mult
+            )
+            nc.vector.scalar_tensor_tensor(
+                out=o_sum_rows[:, b, :],
+                in0=c_centred[:],
+                scalar=c_inverse[0:1, :],
+                in1=bias_row_plus_1[:],
+                op0=ALU.mult,
+                op1=ALU.add,
+            )
+        nc.sync.dma_start(
+            out=out_1.rearrange("(o b) j -> o (b j)", o=1), in_=o_sum_rows[:].rearrange("o b j -> o (b j)")
+        )

@@ -24,10 +24,13 @@ HALVES = N // P
 WORDS = K_PASS // 2
 RUN_PASSES = 2
 RUN_K = RUN_PASSES * K_PASS
-CHUNKS = PASSES // RUN_PASSES
-RUNS = CHUNKS * BATCH
+RUNS = BATCH * PASSES // RUN_PASSES
+CHUNK_RUNS = 2
+CHUNK_K = CHUNK_RUNS * RUN_K
+CHUNK_PASSES = CHUNK_RUNS * RUN_PASSES
+CHUNKS = K // CHUNK_K
 BANK_COLS = 256
-X_BUFS = 8
+X_BUFS = 5
 
 FLOPS = 2 * BATCH * M * K * N + 2 * BATCH * N * M * N
 
@@ -81,29 +84,39 @@ def tile_selfprojection_pa_k_kernel(
             for h in range(HALVES):
                 y_t_sums[b, h] = sums.tile([P, M], F32, name="sum%d%d" % (b, h))
 
-        def load(run):
-            chunk, b = divmod(run, BATCH)
-            xs = x_pool.tile([P, ROW_TILES, RUN_K], BF16)
-            nc.sync.dma_start(
-                out=xs[:],
-                in_=x[b, :, chunk * RUN_K : (chunk + 1) * RUN_K].rearrange("(r t) k -> r t k", t=ROW_TILES),
-            )
-            x_tiles[run] = xs
+        def place(run):
+            chunk, rest = divmod(run, BATCH * CHUNK_RUNS)
+            b, part = divmod(rest, CHUNK_RUNS)
+            return chunk, b, part
+
+        def load(chunk, b):
+            xs = x_pool.tile([P, ROW_TILES, CHUNK_K], BF16)
+            pieces = CHUNK_RUNS if chunk in (0, CHUNKS - 1) else 1
+            width = CHUNK_K // pieces
+            for piece in range(pieces):
+                k0 = chunk * CHUNK_K + piece * width
+                nc.sync.dma_start(
+                    out=xs[:, :, piece * width : (piece + 1) * width],
+                    in_=x[b, :, k0 : k0 + width].rearrange("(r t) k -> r t k", t=ROW_TILES),
+                )
+            x_tiles[chunk, b] = xs
             if b == 0:
-                wj = w_pool.tile([P, RUN_PASSES, N], U32, align_bytes=64)
+                wj = w_pool.tile([P, CHUNK_PASSES, N], U32, align_bytes=64)
                 nc.sync.dma_start(
                     out=wj[:].bitcast(I32),
-                    in_=wj_words[chunk * RUN_PASSES : (chunk + 1) * RUN_PASSES].rearrange("g p n -> p g n"),
+                    in_=wj_words[chunk * CHUNK_PASSES : (chunk + 1) * CHUNK_PASSES].rearrange("g p n -> p g n"),
                 )
                 w_tiles[chunk] = wj
 
         def sort_words(run):
-            xs_words = x_tiles[run][:].bitcast(F32)
+            chunk, b, part = place(run)
+            xs_words = x_tiles[chunk, b][:].bitcast(F32)
             planes = work.tile([P, RUN_PASSES, ROW_TILES, 2, P], F32)
             for g in range(RUN_PASSES):
+                w0 = (part * RUN_PASSES + g) * WORDS
                 nc.vector.tensor_copy(
                     out=planes[:, g],
-                    in_=xs_words[:, :, g * WORDS : (g + 1) * WORDS].rearrange("r t (j u) -> r t u j", u=2),
+                    in_=xs_words[:, :, w0 : w0 + WORDS].rearrange("r t (j u) -> r t u j", u=2),
                 )
             sorted_tiles[run] = planes
 
@@ -140,14 +153,15 @@ def tile_selfprojection_pa_k_kernel(
             code_tiles[run] = (codes, scales)
 
         def multiply(run):
-            chunk, b = divmod(run, BATCH)
+            chunk, b, part = place(run)
             codes, scales = code_tiles[run]
             for g in range(RUN_PASSES):
-                k_pass = chunk * RUN_PASSES + g
+                in_chunk = part * RUN_PASSES + g
+                k_pass = chunk * CHUNK_PASSES + in_chunk
                 for h in range(HALVES):
                     nc.tensor.matmul_mx(
                         out=y_t_sums[b, h][:],
-                        lhsT=w_tiles[chunk][:, g, h * P : (h + 1) * P].bitcast(FP8X4),
+                        lhsT=w_tiles[chunk][:, in_chunk, h * P : (h + 1) * P].bitcast(FP8X4),
                         lhsT_scale=wj_scales[:, k_pass, h * P : (h + 1) * P],
                         rhs=codes[:, g, :].bitcast(FP8X4),
                         rhs_scale=scales[:, g, :],
@@ -156,13 +170,13 @@ def tile_selfprojection_pa_k_kernel(
                     )
 
         with tc.manual_schedule():
-            load(0)
+            load(0, 0)
             wj_scale_rows = original_xj_y_scales.bitcast(I32).rearrange("g (q r) n -> r q g n", r=4)
             for r in range(4):
                 nc.sync.dma_start(out=wj_scales[r:P:32].bitcast(I32), in_=wj_scale_rows[r])
             for step in range(RUNS + 3):
-                if step + 1 < RUNS:
-                    load(step + 1)
+                if step % CHUNK_RUNS == 0 and step + CHUNK_RUNS < RUNS:
+                    load(*place(step + CHUNK_RUNS)[:2])
                 if step < RUNS:
                     sort_words(step)
                 if 0 <= step - 1 < RUNS:

@@ -24,13 +24,11 @@ HALVES = N // P
 WORDS = K_PASS // 2
 RUN_PASSES = 2
 RUN_K = RUN_PASSES * K_PASS
-RUNS = BATCH * PASSES // RUN_PASSES
-CHUNK_RUNS = 2
-CHUNK_K = CHUNK_RUNS * RUN_K
-CHUNK_PASSES = CHUNK_RUNS * RUN_PASSES
-CHUNKS = K // CHUNK_K
+CHUNKS = PASSES // RUN_PASSES
+RUNS = CHUNKS * BATCH
 BANK_COLS = 256
-X_BUFS = 5
+X_BUFS = 8
+EARLY_PASSES = 8
 
 FLOPS = 2 * BATCH * M * K * N + 2 * BATCH * N * M * N
 
@@ -84,39 +82,34 @@ def tile_selfprojection_pa_k_kernel(
             for h in range(HALVES):
                 y_t_sums[b, h] = sums.tile([P, M], F32, name="sum%d%d" % (b, h))
 
-        def place(run):
-            chunk, rest = divmod(run, BATCH * CHUNK_RUNS)
-            b, part = divmod(rest, CHUNK_RUNS)
-            return chunk, b, part
+        def load_wj_scales(first, last):
+            rows = original_xj_y_scales[first:last].bitcast(I32).rearrange("g (q r) n -> r q g n", r=4)
+            for r in range(4):
+                nc.sync.dma_start(out=wj_scales[r:P:32, first:last, :].bitcast(I32), in_=rows[r])
 
-        def load(chunk, b):
-            xs = x_pool.tile([P, ROW_TILES, CHUNK_K], BF16)
-            pieces = CHUNK_RUNS if chunk in (0, CHUNKS - 1) else 1
-            width = CHUNK_K // pieces
-            for piece in range(pieces):
-                k0 = chunk * CHUNK_K + piece * width
-                nc.sync.dma_start(
-                    out=xs[:, :, piece * width : (piece + 1) * width],
-                    in_=x[b, :, k0 : k0 + width].rearrange("(r t) k -> r t k", t=ROW_TILES),
-                )
-            x_tiles[chunk, b] = xs
+        def load(run):
+            chunk, b = divmod(run, BATCH)
+            xs = x_pool.tile([P, ROW_TILES, RUN_K], BF16)
+            nc.sync.dma_start(
+                out=xs[:],
+                in_=x[b, :, chunk * RUN_K : (chunk + 1) * RUN_K].rearrange("(r t) k -> r t k", t=ROW_TILES),
+            )
+            x_tiles[run] = xs
             if b == 0:
-                wj = w_pool.tile([P, CHUNK_PASSES, N], U32, align_bytes=64)
+                wj = w_pool.tile([P, RUN_PASSES, N], U32, align_bytes=64)
                 nc.sync.dma_start(
                     out=wj[:].bitcast(I32),
-                    in_=wj_words[chunk * CHUNK_PASSES : (chunk + 1) * CHUNK_PASSES].rearrange("g p n -> p g n"),
+                    in_=wj_words[chunk * RUN_PASSES : (chunk + 1) * RUN_PASSES].rearrange("g p n -> p g n"),
                 )
                 w_tiles[chunk] = wj
 
         def sort_words(run):
-            chunk, b, part = place(run)
-            xs_words = x_tiles[chunk, b][:].bitcast(F32)
+            xs_words = x_tiles[run][:].bitcast(F32)
             planes = work.tile([P, RUN_PASSES, ROW_TILES, 2, P], F32)
             for g in range(RUN_PASSES):
-                w0 = (part * RUN_PASSES + g) * WORDS
                 nc.vector.tensor_copy(
                     out=planes[:, g],
-                    in_=xs_words[:, :, w0 : w0 + WORDS].rearrange("r t (j u) -> r t u j", u=2),
+                    in_=xs_words[:, :, g * WORDS : (g + 1) * WORDS].rearrange("r t (j u) -> r t u j", u=2),
                 )
             sorted_tiles[run] = planes
 
@@ -153,15 +146,14 @@ def tile_selfprojection_pa_k_kernel(
             code_tiles[run] = (codes, scales)
 
         def multiply(run):
-            chunk, b, part = place(run)
+            chunk, b = divmod(run, BATCH)
             codes, scales = code_tiles[run]
             for g in range(RUN_PASSES):
-                in_chunk = part * RUN_PASSES + g
-                k_pass = chunk * CHUNK_PASSES + in_chunk
+                k_pass = chunk * RUN_PASSES + g
                 for h in range(HALVES):
                     nc.tensor.matmul_mx(
                         out=y_t_sums[b, h][:],
-                        lhsT=w_tiles[chunk][:, in_chunk, h * P : (h + 1) * P].bitcast(FP8X4),
+                        lhsT=w_tiles[chunk][:, g, h * P : (h + 1) * P].bitcast(FP8X4),
                         lhsT_scale=wj_scales[:, k_pass, h * P : (h + 1) * P],
                         rhs=codes[:, g, :].bitcast(FP8X4),
                         rhs_scale=scales[:, g, :],
@@ -170,21 +162,22 @@ def tile_selfprojection_pa_k_kernel(
                     )
 
         with tc.manual_schedule():
-            load(0, 0)
-            wj_scale_rows = original_xj_y_scales.bitcast(I32).rearrange("g (q r) n -> r q g n", r=4)
-            for r in range(4):
-                nc.sync.dma_start(out=wj_scales[r:P:32].bitcast(I32), in_=wj_scale_rows[r])
-            for step in range(RUNS + 3):
-                if step % CHUNK_RUNS == 0 and step + CHUNK_RUNS < RUNS:
-                    load(*place(step + CHUNK_RUNS)[:2])
-                if step < RUNS:
-                    sort_words(step)
-                if 0 <= step - 1 < RUNS:
-                    transpose(step - 1)
-                if 0 <= step - 2 < RUNS:
-                    quantise(step - 2)
-                if 0 <= step - 3 < RUNS:
-                    multiply(step - 3)
+            load(0)
+            load_wj_scales(0, EARLY_PASSES)
+            sort_words(0)
+            for run in range(RUNS + 1):
+                if run + 1 < RUNS:
+                    load(run + 1)
+                if run + 1 == EARLY_PASSES // 2:
+                    load_wj_scales(EARLY_PASSES, PASSES)
+                if run >= 1:
+                    quantise(run - 1)
+                if run + 1 < RUNS:
+                    sort_words(run + 1)
+                if run < RUNS:
+                    transpose(run)
+                if run >= 1:
+                    multiply(run - 1)
 
             wi = const.tile([P, N], U32, align_bytes=64)
             nc.sync.dma_start(
@@ -204,7 +197,9 @@ def tile_selfprojection_pa_k_kernel(
             nc.sync.dma_start(out=bias_row[:], in_=beta_o_sum.rearrange("(o j) -> o j", o=1))
 
         bias_row_plus_1 = const.tile([1, N], F32)
-        nc.vector.tensor_scalar_add(out=bias_row_plus_1[:], in0=bias_row[:], scalar1=1.0)
+        nc.gpsimd.tensor_scalar(
+            out=bias_row_plus_1[:], in0=bias_row[:], scalar1=1.0, scalar2=1.0, op0=ALU.add, op1=ALU.mult
+        )
         o_sum_rows = const.tile([1, BATCH, N], F32)
 
         def one_over_spread(variance, count, label):
@@ -216,18 +211,24 @@ def tile_selfprojection_pa_k_kernel(
             return inverse
 
         for b in range(BATCH):
-            y_t = tail.tile([P, HALVES, M], F32, name="y_t%d" % b)
-            c_cols = []
-            for h in range(HALVES):
-                c_col = tail.tile([P, 1], F32, name="c_col%d%d" % (b, h))
-                nc.scalar.activation(out=y_t[:, h, :], in_=y_t_sums[b, h][:], func=ACT.Copy, accum_out=c_col[:])
-                c_cols.append(c_col)
+            y_t = [tail.tile([P, M], F32, name="y_t%d%d" % (b, h)) for h in range(HALVES)]
+            c_cols = [tail.tile([P, 1], F32, name="c_col%d%d" % (b, h)) for h in range(HALVES)]
+            nc.scalar.activation(out=y_t[0][:], in_=y_t_sums[b, 0][:], func=ACT.Copy, accum_out=c_cols[0][:])
+            nc.vector.tensor_scalar(
+                out=y_t[1][:],
+                in0=y_t_sums[b, 1][:],
+                scalar1=1.0,
+                scalar2=None,
+                op0=ALU.mult,
+                op1=ALU.add,
+                accum_out=c_cols[1][:],
+            )
 
             y_grouped = tail.tile([P, N, PACK], BF16, name="y_grouped%d" % b, align_bytes=64)
             for h in range(HALVES):
                 y_bank = banks.tile([P, PACK, P], F32, tag="bank", name="y_bank%d%d" % (b, h))
                 for t in range(PACK):
-                    nc.tensor.transpose(out=y_bank[:, t, :], in_=y_t[:, h, t * P : (t + 1) * P], identity=ident[:])
+                    nc.tensor.transpose(out=y_bank[:, t, :], in_=y_t[h][:, t * P : (t + 1) * P], identity=ident[:])
                 copy_out = nc.scalar.copy if h == 0 else nc.vector.tensor_copy
                 copy_out(out=y_grouped[:, h * P : (h + 1) * P, :], in_=y_bank[:].rearrange("r t j -> r j t"))
             y_codes = tail.tile([P, N], U32, name="y_codes%d" % b, align_bytes=64)
@@ -250,10 +251,11 @@ def tile_selfprojection_pa_k_kernel(
                 )
 
             z_flat = z[:].rearrange("i h j -> i (h j)")
-            z_stats = tail.tile([P, 6], F32, name="z_stats%d" % b)
-            nc.vector.bn_stats(out=z_stats[:], in_=z_flat)
+            z_stats = tail.tile([P, HALVES, 6], F32, name="z_stats%d" % b)
+            for h in range(HALVES):
+                nc.vector.bn_stats(out=z_stats[:, h, :], in_=z[:, h, :])
             z_mv = tail.tile([P, 2], F32, name="z_mv%d" % b)
-            nc.vector.bn_aggr(out=z_mv[:], in_=z_stats[:])
+            nc.vector.bn_aggr(out=z_mv[:], in_=z_stats[:].rearrange("i h s -> i (h s)"))
             over_all = sums.tile([P, 2], F32, tag="sum%d1" % b, name="over_all%d" % b)
             nc.tensor.matmul(out=over_all[:, 0:1], lhsT=averager[:], rhs=z_mv[:, 0:1], start=True, stop=True)
             z_mean = tail.tile([P, 1], F32, name="z_mean%d" % b)
@@ -300,18 +302,16 @@ def tile_selfprojection_pa_k_kernel(
             c_mv = tail.tile([P, 2], F32, name="c_mv%d" % b)
             nc.vector.bn_aggr(out=c_mv[:], in_=c_stats[:])
             c_inverse = one_over_spread(c_mv[:, 1:2], float(N), "c%d" % b)
-            c_centred = tail.tile([1, N], F32, name="c_centred%d" % b)
-            nc.vector.scalar_tensor_tensor(
-                out=c_centred[:], in0=c_rows[0:1, :], scalar=c_mv[0:1, 0:1], in1=gain_row[:], op0=ALU.subtract, op1=ALU.mult
+            c_shift = tail.tile([P, 1], F32, name="c_shift%d" % b)
+            nc.vector.tensor_scalar(
+                out=c_shift[:], in0=c_mv[:, 0:1], scalar1=c_inverse[:], scalar2=-1.0, op0=ALU.mult, op1=ALU.mult
             )
-            nc.vector.scalar_tensor_tensor(
-                out=o_sum_rows[:, b, :],
-                in0=c_centred[:],
-                scalar=c_inverse[0:1, :],
-                in1=bias_row_plus_1[:],
-                op0=ALU.mult,
-                op1=ALU.add,
+            c_normal = tail.tile([1, N], F32, name="c_normal%d" % b)
+            nc.scalar.activation(
+                out=c_normal[:], in_=c_rows[0:1, :], func=ACT.Identity, scale=c_inverse[0:1, :], bias=c_shift[0:1, :]
             )
+            nc.gpsimd.tensor_tensor(out=c_normal[:], in0=c_normal[:], in1=gain_row[:], op=ALU.mult)
+            nc.gpsimd.tensor_tensor(out=o_sum_rows[:, b, :], in0=c_normal[:], in1=bias_row_plus_1[:], op=ALU.add)
         nc.sync.dma_start(
             out=out_1.rearrange("(o b) j -> o (b j)", o=1), in_=o_sum_rows[:].rearrange("o b j -> o (b j)")
         )

@@ -90,11 +90,18 @@ def tile_selfprojection_pa_k_kernel(
         def load(run):
             chunk, b = divmod(run, BATCH)
             xs = x_pool.tile([P, ROW_TILES, RUN_K], BF16)
-            nc.sync.dma_start(
-                out=xs[:],
-                in_=x[b, :, chunk * RUN_K : (chunk + 1) * RUN_K].rearrange("(r t) k -> r t k", t=ROW_TILES),
-            )
+            piece = K_PASS if run < BATCH else RUN_K
+            for k in range(0, RUN_K, piece):
+                nc.sync.dma_start(
+                    out=xs[:, :, k : k + piece],
+                    in_=x[b, :, chunk * RUN_K + k : chunk * RUN_K + k + piece].rearrange(
+                        "(r t) k -> r t k", t=ROW_TILES
+                    ),
+                )
             x_tiles[run] = xs
+
+        def load_wj(run):
+            chunk, b = divmod(run, BATCH)
             if b == 0:
                 wj = w_pool.tile([P, RUN_PASSES, N], U32, align_bytes=64)
                 nc.sync.dma_start(
@@ -163,11 +170,14 @@ def tile_selfprojection_pa_k_kernel(
 
         with tc.manual_schedule():
             load(0)
+            load(1)
+            load_wj(0)
             load_wj_scales(0, EARLY_PASSES)
             sort_words(0)
             for run in range(RUNS + 1):
-                if run + 1 < RUNS:
+                if 1 < run + 1 < RUNS:
                     load(run + 1)
+                    load_wj(run + 1)
                 if run + 1 == EARLY_PASSES // 2:
                     load_wj_scales(EARLY_PASSES, PASSES)
                 if run >= 1:

@@ -26,6 +26,7 @@ RUN_PASSES = 2
 RUN_K = RUN_PASSES * K_PASS
 CHUNKS = PASSES // RUN_PASSES
 RUNS = CHUNKS * BATCH
+RUN_LIST = [divmod(run, BATCH) for run in range(RUNS)]
 BANK_COLS = 256
 X_BUFS = 8
 EARLY_PASSES = 8
@@ -82,26 +83,21 @@ def tile_selfprojection_pa_k_kernel(
             for h in range(HALVES):
                 y_t_sums[b, h] = sums.tile([P, M], F32, name="sum%d%d" % (b, h))
 
-        def load_wj_scales(first, last):
+        def load_wj_scales(first, last, r):
             rows = original_xj_y_scales[first:last].bitcast(I32).rearrange("g (q r) n -> r q g n", r=4)
-            for r in range(4):
-                nc.sync.dma_start(out=wj_scales[r:P:32, first:last, :].bitcast(I32), in_=rows[r])
+            nc.sync.dma_start(out=wj_scales[r:P:32, first:last, :].bitcast(I32), in_=rows[r])
 
         def load(run):
             chunk, b = divmod(run, BATCH)
-            xs = x_pool.tile([P, ROW_TILES, RUN_K], BF16)
-            piece = K_PASS if run < BATCH else RUN_K
-            for k in range(0, RUN_K, piece):
-                nc.sync.dma_start(
-                    out=xs[:, :, k : k + piece],
-                    in_=x[b, :, chunk * RUN_K + k : chunk * RUN_K + k + piece].rearrange(
-                        "(r t) k -> r t k", t=ROW_TILES
-                    ),
-                )
+            xs = x_pool.tile([P, ROW_TILES, RUN_K], BF16, name="xs")
+            nc.sync.dma_start(
+                out=xs[:],
+                in_=x[b, :, chunk * RUN_K : (chunk + 1) * RUN_K].rearrange("(r t) k -> r t k", t=ROW_TILES),
+            )
             x_tiles[run] = xs
 
         def load_wj(run):
-            chunk, b = divmod(run, BATCH)
+            chunk, b = RUN_LIST[run]
             if b == 0:
                 wj = w_pool.tile([P, RUN_PASSES, N], U32, align_bytes=64)
                 nc.sync.dma_start(
@@ -153,7 +149,7 @@ def tile_selfprojection_pa_k_kernel(
             code_tiles[run] = (codes, scales)
 
         def multiply(run):
-            chunk, b = divmod(run, BATCH)
+            chunk, b = RUN_LIST[run]
             codes, scales = code_tiles[run]
             for g in range(RUN_PASSES):
                 k_pass = chunk * RUN_PASSES + g
@@ -168,18 +164,187 @@ def tile_selfprojection_pa_k_kernel(
                         stop=(k_pass == PASSES - 1),
                     )
 
+        wi = const.tile([P, N], U32, name="wi", align_bytes=64)
+        gain = const.tile([P, HALVES, N], BF16, name="gain")
+        bias = const.tile([P, HALVES, N], BF16, name="bias")
+        gain_row = const.tile([1, N], BF16, name="gain_row")
+        bias_row = const.tile([1, N], BF16, name="bias_row")
+        bias_row_plus_1 = const.tile([1, N], F32, name="bias_row_plus_1")
+        o_sum_rows = const.tile([1, BATCH, N], F32, name="o_sum_rows")
+        y_t, c_cols, y_grouped, y_coded, z, c_rows, centred = [{} for i in range(7)]
+        c_mv = tail.tile([P, 2, BATCH], F32, name="c_mv")
+        z_mv = tail.tile([P, 2, BATCH], F32, name="z_mv")
+
+        wi_scale_rows = original_xi_y_scales.bitcast(I32).rearrange("g (q r) n -> r (g q) n", r=4)
+        end_inputs = [
+            (wi[:].bitcast(I32), original_xi_y_words.rearrange("g p n t -> (g p) (n t)").bitcast(I32)),
+            (gain[:], gamma_o.rearrange("(h i) j -> i h j", h=HALVES)),
+            (bias[:], beta_o.rearrange("(h i) j -> i h j", h=HALVES)),
+            (gain_row[:], gamma_o_sum.rearrange("(o j) -> o j", o=1)),
+            (bias_row[:], beta_o_sum.rearrange("(o j) -> o j", o=1)),
+        ]
+        end_inputs.extend([(wi_scales[r:P:32].bitcast(I32), wi_scale_rows[r]) for r in range(4)])
+
+        def copy_y_out(b):
+            for h in range(HALVES):
+                y_t[b, h] = tail.tile([P, 2, P, 2], BF16, name="y_t%d%d" % (b, h))
+                c_cols[b, h] = tail.tile([P, 1], F32, name="c_col%d%d" % (b, h))
+                y_rows = y_t_sums[b, h][:].rearrange("n (u e r) -> n u r e", u=2, e=2)
+                if h == 0:
+                    nc.scalar.activation(out=y_t[b, h][:], in_=y_rows, func=ACT.Copy, accum_out=c_cols[b, h][:])
+                else:
+                    nc.vector.tensor_scalar(
+                        out=y_t[b, h][:],
+                        in0=y_rows,
+                        scalar1=1.0,
+                        scalar2=None,
+                        op0=ALU.mult,
+                        op1=ALU.add,
+                        accum_out=c_cols[b, h][:],
+                    )
+
+        def turn_y(b):
+            y_grouped[b] = tail.tile([P, N, PACK], BF16, name="y_grouped%d" % b, align_bytes=64)
+            y_words = y_grouped[b][:].bitcast(F32)
+            y_banks = []
+            for h in range(HALVES):
+                y_bank = sums.tile([P, 2, P], F32, tag="sum%d%d" % (b, h), name="y_bank%d%d" % (b, h))
+                columns = y_t[b, h][:].rearrange("n u r e -> n (u r e)").bitcast(F32)
+                for u in range(2):
+                    nc.tensor.transpose(out=y_bank[:, u, :], in_=columns[:, u * P : (u + 1) * P], identity=ident[:])
+                y_banks.append(y_bank)
+            c_rows[b] = banks.tile([P, N], F32, tag="bank", name="c_rows%d" % b)
+            for h in range(HALVES):
+                nc.tensor.transpose(
+                    out=c_rows[b][:, h * P : (h + 1) * P], in_=c_cols[b, h][:].to_broadcast([P, P]), identity=ident[:]
+                )
+            for h in range(HALVES):
+                nc.scalar.copy(out=y_words[:, h * P : (h + 1) * P, :], in_=y_banks[h][:].rearrange("r u n -> r n u"))
+
+        def c_statistics(b):
+            c_stats = tail.tile([P, 6], F32, name="c_stats%d" % b)
+            nc.vector.bn_stats(out=c_stats[:], in_=c_rows[b][:])
+            nc.vector.bn_aggr(out=c_mv[:, :, b], in_=c_stats[:])
+
+        def quantise_y(b):
+            y_codes = tail.tile([P, N], U32, name="y_codes%d" % b, align_bytes=64)
+            y_scales = tail.tile([P, N], U8, name="y_scales%d" % b, align_bytes=64)
+            nc.vector.quantize_mx(
+                out=y_codes[:].bitcast(FP8X4),
+                scales=y_scales[:],
+                in_=y_grouped[b][:].rearrange("r j t -> r (j t)"),
+            )
+            y_coded[b] = (y_codes, y_scales)
+
+        def multiply_y(b):
+            y_codes, y_scales = y_coded[b]
+            z[b] = sums.tile([P, HALVES, N], F32, tag="sum%d0" % b, name="z%d" % b)
+            for h in range(HALVES):
+                nc.tensor.matmul_mx(
+                    out=z[b][:, h, :],
+                    lhsT=wi[:, h * P : (h + 1) * P].bitcast(FP8X4),
+                    lhsT_scale=wi_scales[:, h * P : (h + 1) * P],
+                    rhs=y_codes[:].bitcast(FP8X4),
+                    rhs_scale=y_scales[:],
+                    start=True,
+                    stop=True,
+                )
+
+        def z_statistics(b):
+            z_stats = tail.tile([P, 6], F32, name="z_stats%d" % b)
+            nc.vector.bn_stats(out=z_stats[:], in_=z[b][:].rearrange("i h j -> i (h j)"))
+            nc.vector.bn_aggr(out=z_mv[:, :, b], in_=z_stats[:])
+
+        def inverse_spread(variance, count, label):
+            spread = tail.tile([P, BATCH], F32, name="spread_" + label)
+            nc.scalar.activation(out=spread[:], in_=variance, func=ACT.Sqrt, scale=count / (count - 1.0))
+            nc.vector.tensor_scalar_add(out=spread[:], in0=spread[:], scalar1=EPS)
+            inverse = tail.tile([P, BATCH], F32, name="inverse_" + label)
+            nc.vector.reciprocal(out=inverse[:], in_=spread[:])
+            return inverse
+
+        def normalise_c(inverse):
+            shift = tail.tile([P, BATCH], F32, name="c_shift")
+            nc.vector.scalar_tensor_tensor(
+                out=shift[:], in0=c_mv[:, 0, :], scalar=-1.0, in1=inverse[:], op0=ALU.mult, op1=ALU.mult
+            )
+            for b in range(BATCH):
+                c_normal = tail.tile([1, N], F32, name="c_normal%d" % b)
+                nc.scalar.activation(
+                    out=c_normal[:],
+                    in_=c_rows[b][0:1, :],
+                    func=ACT.Identity,
+                    scale=inverse[0:1, b : b + 1],
+                    bias=shift[0:1, b : b + 1],
+                )
+                nc.gpsimd.tensor_tensor(out=c_normal[:], in0=c_normal[:], in1=gain_row[:], op=ALU.mult)
+                nc.gpsimd.tensor_tensor(
+                    out=o_sum_rows[:, b, :], in0=c_normal[:], in1=bias_row_plus_1[:], op=ALU.add
+                )
+
+        def finish():
+            for b in range(BATCH):
+                copy_y_out(b)
+            for b in range(BATCH):
+                turn_y(b)
+            for b in range(BATCH):
+                c_statistics(b)
+            for b in range(BATCH):
+                quantise_y(b)
+                multiply_y(b)
+            normalise_c(inverse_spread(c_mv[:, 1, :], float(N), "c"))
+            nc.sync.dma_start(
+                out=out_1.rearrange("(o b) j -> o (b j)", o=1), in_=o_sum_rows[:].rearrange("o b j -> o (b j)")
+            )
+            for b in range(BATCH):
+                z_statistics(b)
+            means = banks.tile([P, 2, BATCH], F32, tag="bank", name="means")
+            nc.tensor.matmul(out=means[:, 0, :], lhsT=averager[:], rhs=z_mv[:, 0, :], start=True, stop=True)
+            distance = tail.tile([P, BATCH], F32, name="distance")
+            nc.vector.tensor_sub(out=distance[:], in0=z_mv[:, 0, :], in1=means[:, 0, :])
+            part_var = tail.tile([P, BATCH], F32, name="part_var")
+            nc.vector.tensor_mul(out=part_var[:], in0=distance[:], in1=distance[:])
+            nc.vector.tensor_add(out=part_var[:], in0=part_var[:], in1=z_mv[:, 1, :])
+            z_mean = tail.tile([P, BATCH], F32, name="z_mean")
+            nc.vector.tensor_copy(out=z_mean[:], in_=means[:, 0, :])
+            nc.tensor.matmul(out=means[:, 1, :], lhsT=averager[:], rhs=part_var[:], start=True, stop=True)
+            for b in range(BATCH):
+                centred[b] = tail.tile([P, HALVES * N], F32, name="centred%d" % b)
+                nc.vector.scalar_tensor_tensor(
+                    out=centred[b][:],
+                    in0=z[b][:].rearrange("i h j -> i (h j)"),
+                    scalar=z_mean[:, b : b + 1],
+                    in1=gain[:].rearrange("i h j -> i (h j)"),
+                    op0=ALU.subtract,
+                    op1=ALU.mult,
+                )
+            inverse = inverse_spread(means[:, 1, :], float(N * N), "z")
+            for b in range(BATCH):
+                result = tail.tile([P, HALVES, N], F32, name="result%d" % b)
+                nc.vector.scalar_tensor_tensor(
+                    out=result[:].rearrange("i h j -> i (h j)"),
+                    in0=centred[b][:],
+                    scalar=inverse[:, b : b + 1],
+                    in1=bias[:].rearrange("i h j -> i (h j)"),
+                    op0=ALU.mult,
+                    op1=ALU.add,
+                )
+                nc.sync.dma_start(out=out_0[b].rearrange("(h i) j -> i h j", h=HALVES), in_=result[:])
+
         with tc.manual_schedule():
             load(0)
             load(1)
             load_wj(0)
-            load_wj_scales(0, EARLY_PASSES)
+            for r in range(4):
+                load_wj_scales(0, EARLY_PASSES, r)
             sort_words(0)
             for run in range(RUNS + 1):
                 if 1 < run + 1 < RUNS:
                     load(run + 1)
-                    load_wj(run + 1)
-                if run + 1 == EARLY_PASSES // 2:
-                    load_wj_scales(EARLY_PASSES, PASSES)
+                if 1 <= run < RUNS:
+                    load_wj(run)
+                if 3 <= run < 7:
+                    load_wj_scales(EARLY_PASSES, PASSES, run - 3)
                 if run >= 1:
                     quantise(run - 1)
                 if run + 1 < RUNS:
@@ -189,139 +354,10 @@ def tile_selfprojection_pa_k_kernel(
                 if run >= 1:
                     multiply(run - 1)
 
-            wi = const.tile([P, N], U32, align_bytes=64)
-            nc.sync.dma_start(
-                out=wi[:].bitcast(I32),
-                in_=original_xi_y_words.rearrange("g p n t -> (g p) (n t)").bitcast(I32),
-            )
-            wi_scale_rows = original_xi_y_scales.bitcast(I32).rearrange("g (q r) n -> r (g q) n", r=4)
-            for r in range(4):
-                nc.sync.dma_start(out=wi_scales[r:P:32].bitcast(I32), in_=wi_scale_rows[r])
-            gain = const.tile([P, HALVES, N], BF16)
-            nc.sync.dma_start(out=gain[:], in_=gamma_o.rearrange("(h i) j -> i h j", h=HALVES))
-            bias = const.tile([P, HALVES, N], BF16)
-            nc.sync.dma_start(out=bias[:], in_=beta_o.rearrange("(h i) j -> i h j", h=HALVES))
-            gain_row = const.tile([1, N], BF16)
-            nc.sync.dma_start(out=gain_row[:], in_=gamma_o_sum.rearrange("(o j) -> o j", o=1))
-            bias_row = const.tile([1, N], BF16)
-            nc.sync.dma_start(out=bias_row[:], in_=beta_o_sum.rearrange("(o j) -> o j", o=1))
-
-        bias_row_plus_1 = const.tile([1, N], F32)
-        nc.gpsimd.tensor_scalar(
-            out=bias_row_plus_1[:], in0=bias_row[:], scalar1=1.0, scalar2=1.0, op0=ALU.add, op1=ALU.mult
-        )
-        o_sum_rows = const.tile([1, BATCH, N], F32)
-
-        def one_over_spread(variance, count, label):
-            spread = tail.tile([P, 1], F32, name="spread_" + label)
-            nc.scalar.activation(out=spread[:], in_=variance, func=ACT.Sqrt, scale=count / (count - 1.0))
-            nc.vector.tensor_scalar_add(out=spread[:], in0=spread[:], scalar1=EPS)
-            inverse = tail.tile([P, 1], F32, name="inverse_" + label)
-            nc.vector.reciprocal(out=inverse[:], in_=spread[:])
-            return inverse
-
-        for b in range(BATCH):
-            y_t = [tail.tile([P, M], F32, name="y_t%d%d" % (b, h)) for h in range(HALVES)]
-            c_cols = [tail.tile([P, 1], F32, name="c_col%d%d" % (b, h)) for h in range(HALVES)]
-            nc.scalar.activation(out=y_t[0][:], in_=y_t_sums[b, 0][:], func=ACT.Copy, accum_out=c_cols[0][:])
-            nc.vector.tensor_scalar(
-                out=y_t[1][:],
-                in0=y_t_sums[b, 1][:],
-                scalar1=1.0,
-                scalar2=None,
-                op0=ALU.mult,
-                op1=ALU.add,
-                accum_out=c_cols[1][:],
+            for target, source in end_inputs:
+                nc.sync.dma_start(out=target, in_=source)
+            nc.gpsimd.tensor_scalar(
+                out=bias_row_plus_1[:], in0=bias_row[:], scalar1=1.0, scalar2=1.0, op0=ALU.add, op1=ALU.mult
             )
 
-            y_grouped = tail.tile([P, N, PACK], BF16, name="y_grouped%d" % b, align_bytes=64)
-            for h in range(HALVES):
-                y_bank = banks.tile([P, PACK, P], F32, tag="bank", name="y_bank%d%d" % (b, h))
-                for t in range(PACK):
-                    nc.tensor.transpose(out=y_bank[:, t, :], in_=y_t[h][:, t * P : (t + 1) * P], identity=ident[:])
-                copy_out = nc.scalar.copy if h == 0 else nc.vector.tensor_copy
-                copy_out(out=y_grouped[:, h * P : (h + 1) * P, :], in_=y_bank[:].rearrange("r t j -> r j t"))
-            y_codes = tail.tile([P, N], U32, name="y_codes%d" % b, align_bytes=64)
-            y_scales = tail.tile([P, N], U8, name="y_scales%d" % b, align_bytes=64)
-            nc.vector.quantize_mx(
-                out=y_codes[:].bitcast(FP8X4),
-                scales=y_scales[:],
-                in_=y_grouped[:].rearrange("r j t -> r (j t)"),
-            )
-            z = sums.tile([P, HALVES, N], F32, tag="sum%d0" % b, name="z%d" % b)
-            for h in range(HALVES):
-                nc.tensor.matmul_mx(
-                    out=z[:, h, :],
-                    lhsT=wi[:, h * P : (h + 1) * P].bitcast(FP8X4),
-                    lhsT_scale=wi_scales[:, h * P : (h + 1) * P],
-                    rhs=y_codes[:].bitcast(FP8X4),
-                    rhs_scale=y_scales[:],
-                    start=True,
-                    stop=True,
-                )
-
-            z_flat = z[:].rearrange("i h j -> i (h j)")
-            z_stats = tail.tile([P, HALVES, 6], F32, name="z_stats%d" % b)
-            for h in range(HALVES):
-                nc.vector.bn_stats(out=z_stats[:, h, :], in_=z[:, h, :])
-            z_mv = tail.tile([P, 2], F32, name="z_mv%d" % b)
-            nc.vector.bn_aggr(out=z_mv[:], in_=z_stats[:].rearrange("i h s -> i (h s)"))
-            over_all = sums.tile([P, 2], F32, tag="sum%d1" % b, name="over_all%d" % b)
-            nc.tensor.matmul(out=over_all[:, 0:1], lhsT=averager[:], rhs=z_mv[:, 0:1], start=True, stop=True)
-            z_mean = tail.tile([P, 1], F32, name="z_mean%d" % b)
-            nc.vector.tensor_copy(out=z_mean[:], in_=over_all[:, 0:1])
-            distance = tail.tile([P, 1], F32, name="distance%d" % b)
-            nc.vector.tensor_sub(out=distance[:], in0=z_mv[:, 0:1], in1=z_mean[:])
-            part_var = tail.tile([P, 1], F32, name="part_var%d" % b)
-            nc.vector.scalar_tensor_tensor(
-                out=part_var[:], in0=distance[:], scalar=distance[:], in1=z_mv[:, 1:2], op0=ALU.mult, op1=ALU.add
-            )
-            nc.tensor.matmul(out=over_all[:, 1:2], lhsT=averager[:], rhs=part_var[:], start=True, stop=True)
-            centred = tail.tile([P, HALVES * N], F32, name="centred%d" % b)
-            nc.vector.scalar_tensor_tensor(
-                out=centred[:],
-                in0=z_flat,
-                scalar=z_mean[:],
-                in1=gain[:].rearrange("i h j -> i (h j)"),
-                op0=ALU.subtract,
-                op1=ALU.mult,
-            )
-            z_inverse = one_over_spread(over_all[:, 1:2], float(N * N), "z%d" % b)
-            result = tail.tile([P, HALVES, N], F32, name="result%d" % b)
-            nc.vector.scalar_tensor_tensor(
-                out=result[:].rearrange("i h j -> i (h j)"),
-                in0=centred[:],
-                scalar=z_inverse[:],
-                in1=bias[:].rearrange("i h j -> i (h j)"),
-                op0=ALU.mult,
-                op1=ALU.add,
-            )
-            nc.sync.dma_start(out=out_0[b].rearrange("(h i) j -> i h j", h=HALVES), in_=result[:])
-
-            c_rows = banks.tile([P, N], F32, tag="bank", name="c_rows%d" % b)
-            for h in range(HALVES):
-                nc.tensor.matmul(
-                    out=c_rows[:, h * P : (h + 1) * P],
-                    lhsT=c_cols[h][:].to_broadcast([P, P]),
-                    rhs=ident[:],
-                    start=True,
-                    stop=True,
-                )
-            c_stats = tail.tile([P, 6], F32, name="c_stats%d" % b)
-            nc.vector.bn_stats(out=c_stats[:], in_=c_rows[:])
-            c_mv = tail.tile([P, 2], F32, name="c_mv%d" % b)
-            nc.vector.bn_aggr(out=c_mv[:], in_=c_stats[:])
-            c_inverse = one_over_spread(c_mv[:, 1:2], float(N), "c%d" % b)
-            c_shift = tail.tile([P, 1], F32, name="c_shift%d" % b)
-            nc.vector.tensor_scalar(
-                out=c_shift[:], in0=c_mv[:, 0:1], scalar1=c_inverse[:], scalar2=-1.0, op0=ALU.mult, op1=ALU.mult
-            )
-            c_normal = tail.tile([1, N], F32, name="c_normal%d" % b)
-            nc.scalar.activation(
-                out=c_normal[:], in_=c_rows[0:1, :], func=ACT.Identity, scale=c_inverse[0:1, :], bias=c_shift[0:1, :]
-            )
-            nc.gpsimd.tensor_tensor(out=c_normal[:], in0=c_normal[:], in1=gain_row[:], op=ALU.mult)
-            nc.gpsimd.tensor_tensor(out=o_sum_rows[:, b, :], in0=c_normal[:], in1=bias_row_plus_1[:], op=ALU.add)
-        nc.sync.dma_start(
-            out=out_1.rearrange("(o b) j -> o (b j)", o=1), in_=o_sum_rows[:].rearrange("o b j -> o (b j)")
-        )
+            finish()

@@ -130,7 +130,8 @@ def tile_selfprojection_pa_k_kernel(
                                 in_=planes[:, g, c * (BANK_COLS // P) + i, u, :],
                                 identity=ident[:],
                             )
-                    nc.scalar.copy(
+                    copy_out = nc.vector.tensor_copy if (run, g, c) == (RUNS - 1, 1, 0) else nc.scalar.copy
+                    copy_out(
                         out=grouped_words[:, g, c * BANK_COLS : (c + 1) * BANK_COLS, :],
                         in_=bank[:].rearrange("p u m -> p m u"),
                     )
@@ -167,31 +168,35 @@ def tile_selfprojection_pa_k_kernel(
         wi = const.tile([P, N], U32, name="wi", align_bytes=64)
         gain = const.tile([P, HALVES, N], BF16, name="gain")
         bias = const.tile([P, HALVES, N], BF16, name="bias")
-        gain_row = const.tile([1, N], BF16, name="gain_row")
-        bias_row = const.tile([1, N], BF16, name="bias_row")
-        bias_row_plus_1 = const.tile([1, N], F32, name="bias_row_plus_1")
-        o_sum_rows = const.tile([1, BATCH, N], F32, name="o_sum_rows")
-        y_t, c_cols, y_grouped, y_coded, z, c_rows, centred = [{} for i in range(7)]
-        c_mv = tail.tile([P, 2, BATCH], F32, name="c_mv")
-        z_mv = tail.tile([P, 2, BATCH], F32, name="z_mv")
+        c_gain = const.tile([BATCH * HALVES, P], BF16, name="c_gain")
+        c_bias = const.tile([BATCH * HALVES, P], BF16, name="c_bias")
+        c_bias_plus_1 = const.tile([BATCH * HALVES, P], F32, name="c_bias_plus_1")
+        c_wide = const.tile([P, P], F32, name="c_wide")
+        nc.vector.memset(c_wide[:], 0.0)
 
         wi_scale_rows = original_xi_y_scales.bitcast(I32).rearrange("g (q r) n -> r (g q) n", r=4)
         end_inputs = [
             (wi[:].bitcast(I32), original_xi_y_words.rearrange("g p n t -> (g p) (n t)").bitcast(I32)),
-            (gain[:], gamma_o.rearrange("(h i) j -> i h j", h=HALVES)),
-            (bias[:], beta_o.rearrange("(h i) j -> i h j", h=HALVES)),
-            (gain_row[:], gamma_o_sum.rearrange("(o j) -> o j", o=1)),
-            (bias_row[:], beta_o_sum.rearrange("(o j) -> o j", o=1)),
         ]
         end_inputs.extend([(wi_scales[r:P:32].bitcast(I32), wi_scale_rows[r]) for r in range(4)])
+        end_inputs.append((gain[:], gamma_o.rearrange("(h i) j -> i h j", h=HALVES)))
+        end_inputs.append((bias[:], beta_o.rearrange("(h i) j -> i h j", h=HALVES)))
+        for b in range(BATCH):
+            rows = slice(b * HALVES, (b + 1) * HALVES)
+            end_inputs.append((c_gain[rows, :], gamma_o_sum.rearrange("(h n) -> h n", h=HALVES)))
+            end_inputs.append((c_bias[rows, :], beta_o_sum.rearrange("(h n) -> h n", h=HALVES)))
+
+        y_t, y_grouped, y_coded, z, centred = [{} for i in range(5)]
+        c_cols = tail.tile([P, BATCH, HALVES], F32, name="c_cols")
+        z_mv = tail.tile([P, 2, BATCH], F32, name="z_mv")
 
         def copy_y_out(b):
             for h in range(HALVES):
                 y_t[b, h] = tail.tile([P, 2, P, 2], BF16, name="y_t%d%d" % (b, h))
-                c_cols[b, h] = tail.tile([P, 1], F32, name="c_col%d%d" % (b, h))
                 y_rows = y_t_sums[b, h][:].rearrange("n (u e r) -> n u r e", u=2, e=2)
+                c_col = c_cols[:, b, h : h + 1]
                 if h == 0:
-                    nc.scalar.activation(out=y_t[b, h][:], in_=y_rows, func=ACT.Copy, accum_out=c_cols[b, h][:])
+                    nc.scalar.activation(out=y_t[b, h][:], in_=y_rows, func=ACT.Copy, accum_out=c_col)
                 else:
                     nc.vector.tensor_scalar(
                         out=y_t[b, h][:],
@@ -200,31 +205,19 @@ def tile_selfprojection_pa_k_kernel(
                         scalar2=None,
                         op0=ALU.mult,
                         op1=ALU.add,
-                        accum_out=c_cols[b, h][:],
+                        accum_out=c_col,
                     )
 
         def turn_y(b):
             y_grouped[b] = tail.tile([P, N, PACK], BF16, name="y_grouped%d" % b, align_bytes=64)
             y_words = y_grouped[b][:].bitcast(F32)
-            y_banks = []
             for h in range(HALVES):
                 y_bank = sums.tile([P, 2, P], F32, tag="sum%d%d" % (b, h), name="y_bank%d%d" % (b, h))
                 columns = y_t[b, h][:].rearrange("n u r e -> n (u r e)").bitcast(F32)
                 for u in range(2):
                     nc.tensor.transpose(out=y_bank[:, u, :], in_=columns[:, u * P : (u + 1) * P], identity=ident[:])
-                y_banks.append(y_bank)
-            c_rows[b] = banks.tile([P, N], F32, tag="bank", name="c_rows%d" % b)
-            for h in range(HALVES):
-                nc.tensor.transpose(
-                    out=c_rows[b][:, h * P : (h + 1) * P], in_=c_cols[b, h][:].to_broadcast([P, P]), identity=ident[:]
-                )
-            for h in range(HALVES):
-                nc.scalar.copy(out=y_words[:, h * P : (h + 1) * P, :], in_=y_banks[h][:].rearrange("r u n -> r n u"))
-
-        def c_statistics(b):
-            c_stats = tail.tile([P, 6], F32, name="c_stats%d" % b)
-            nc.vector.bn_stats(out=c_stats[:], in_=c_rows[b][:])
-            nc.vector.bn_aggr(out=c_mv[:, :, b], in_=c_stats[:])
+                copy_out = nc.scalar.copy if h == 0 else nc.vector.tensor_copy
+                copy_out(out=y_words[:, h * P : (h + 1) * P, :], in_=y_bank[:].rearrange("r u n -> r n u"))
 
         def quantise_y(b):
             y_codes = tail.tile([P, N], U32, name="y_codes%d" % b, align_bytes=64)
@@ -255,59 +248,76 @@ def tile_selfprojection_pa_k_kernel(
             nc.vector.bn_stats(out=z_stats[:], in_=z[b][:].rearrange("i h j -> i (h j)"))
             nc.vector.bn_aggr(out=z_mv[:, :, b], in_=z_stats[:])
 
-        def inverse_spread(variance, count, label):
-            spread = tail.tile([P, BATCH], F32, name="spread_" + label)
-            nc.scalar.activation(out=spread[:], in_=variance, func=ACT.Sqrt, scale=count / (count - 1.0))
+        def sum_of_halves(columns, name):
+            total = banks.tile([P, BATCH], F32, tag="bank", name=name)
+            for h in range(HALVES):
+                nc.tensor.matmul(
+                    out=total[:], lhsT=averager[:], rhs=columns[:, :, h], start=(h == 0), stop=(h == HALVES - 1)
+                )
+            return total
+
+        def inverse_of(spread, name):
             nc.vector.tensor_scalar_add(out=spread[:], in0=spread[:], scalar1=EPS)
-            inverse = tail.tile([P, BATCH], F32, name="inverse_" + label)
+            inverse = tail.tile([P, BATCH], F32, name=name)
             nc.vector.reciprocal(out=inverse[:], in_=spread[:])
             return inverse
-
-        def normalise_c(inverse):
-            shift = tail.tile([P, BATCH], F32, name="c_shift")
-            nc.vector.scalar_tensor_tensor(
-                out=shift[:], in0=c_mv[:, 0, :], scalar=-1.0, in1=inverse[:], op0=ALU.mult, op1=ALU.mult
-            )
-            for b in range(BATCH):
-                c_normal = tail.tile([1, N], F32, name="c_normal%d" % b)
-                nc.scalar.activation(
-                    out=c_normal[:],
-                    in_=c_rows[b][0:1, :],
-                    func=ACT.Identity,
-                    scale=inverse[0:1, b : b + 1],
-                    bias=shift[0:1, b : b + 1],
-                )
-                nc.gpsimd.tensor_tensor(out=c_normal[:], in0=c_normal[:], in1=gain_row[:], op=ALU.mult)
-                nc.gpsimd.tensor_tensor(
-                    out=o_sum_rows[:, b, :], in0=c_normal[:], in1=bias_row_plus_1[:], op=ALU.add
-                )
 
         def finish():
             for b in range(BATCH):
                 copy_y_out(b)
             for b in range(BATCH):
                 turn_y(b)
-            for b in range(BATCH):
-                c_statistics(b)
+            c_total = sum_of_halves(c_cols, "c_total")
+            c_mean = tail.tile([P, BATCH], F32, name="c_mean")
+            nc.scalar.mul(out=c_mean[:], in_=c_total[:], mul=1.0 / HALVES)
+            c_distance = tail.tile([P, BATCH, HALVES], F32, name="c_distance")
+            nc.gpsimd.tensor_tensor(
+                out=c_distance[:],
+                in0=c_cols[:],
+                in1=c_mean[:].unsqueeze(2).to_broadcast([P, BATCH, HALVES]),
+                op=ALU.subtract,
+            )
+            c_square = tail.tile([P, BATCH, HALVES], F32, name="c_square")
+            nc.gpsimd.tensor_tensor(out=c_square[:], in0=c_distance[:], in1=c_distance[:], op=ALU.mult)
             for b in range(BATCH):
                 quantise_y(b)
                 multiply_y(b)
-            normalise_c(inverse_spread(c_mv[:, 1, :], float(N), "c"))
-            nc.sync.dma_start(
-                out=out_1.rearrange("(o b) j -> o (b j)", o=1), in_=o_sum_rows[:].rearrange("o b j -> o (b j)")
+            c_spread = tail.tile([P, BATCH], F32, name="c_spread")
+            nc.scalar.activation(
+                out=c_spread[:],
+                in_=sum_of_halves(c_square, "c_squares")[:],
+                func=ACT.Sqrt,
+                scale=1.0 / HALVES * N / (N - 1.0),
             )
             for b in range(BATCH):
                 z_statistics(b)
             means = banks.tile([P, 2, BATCH], F32, tag="bank", name="means")
             nc.tensor.matmul(out=means[:, 0, :], lhsT=averager[:], rhs=z_mv[:, 0, :], start=True, stop=True)
+            c_inverse = inverse_of(c_spread, "c_inverse")
+            nc.gpsimd.tensor_tensor(
+                out=c_wide[:, 0 : BATCH * HALVES].rearrange("n (b h) -> n b h", h=HALVES),
+                in0=c_distance[:],
+                in1=c_inverse[:].unsqueeze(2).to_broadcast([P, BATCH, HALVES]),
+                op=ALU.mult,
+            )
             distance = tail.tile([P, BATCH], F32, name="distance")
             nc.vector.tensor_sub(out=distance[:], in0=z_mv[:, 0, :], in1=means[:, 0, :])
             part_var = tail.tile([P, BATCH], F32, name="part_var")
             nc.vector.tensor_mul(out=part_var[:], in0=distance[:], in1=distance[:])
             nc.vector.tensor_add(out=part_var[:], in0=part_var[:], in1=z_mv[:, 1, :])
             z_mean = tail.tile([P, BATCH], F32, name="z_mean")
-            nc.vector.tensor_copy(out=z_mean[:], in_=means[:, 0, :])
+            nc.scalar.copy(out=z_mean[:], in_=means[:, 0, :])
             nc.tensor.matmul(out=means[:, 1, :], lhsT=averager[:], rhs=part_var[:], start=True, stop=True)
+            z_spread = tail.tile([P, BATCH], F32, name="z_spread")
+            nc.scalar.activation(
+                out=z_spread[:], in_=means[:, 1, :], func=ACT.Sqrt, scale=N * N / (N * N - 1.0)
+            )
+            c_bank = banks.tile([P, P], F32, tag="bank", name="c_bank")
+            nc.tensor.transpose(out=c_bank[:], in_=c_wide[:], identity=ident[:])
+            o_sum_rows = tail.tile([BATCH * HALVES, P], F32, name="o_sum_rows")
+            nc.scalar.copy(out=o_sum_rows[:], in_=c_bank[0 : BATCH * HALVES, :])
+            nc.gpsimd.tensor_tensor(out=o_sum_rows[:], in0=o_sum_rows[:], in1=c_gain[:], op=ALU.mult)
+            nc.gpsimd.tensor_tensor(out=o_sum_rows[:], in0=o_sum_rows[:], in1=c_bias_plus_1[:], op=ALU.add)
             for b in range(BATCH):
                 centred[b] = tail.tile([P, HALVES * N], F32, name="centred%d" % b)
                 nc.vector.scalar_tensor_tensor(
@@ -318,18 +328,20 @@ def tile_selfprojection_pa_k_kernel(
                     op0=ALU.subtract,
                     op1=ALU.mult,
                 )
-            inverse = inverse_spread(means[:, 1, :], float(N * N), "z")
+            z_inverse = inverse_of(z_spread, "z_inverse")
             for b in range(BATCH):
                 result = tail.tile([P, HALVES, N], F32, name="result%d" % b)
                 nc.vector.scalar_tensor_tensor(
                     out=result[:].rearrange("i h j -> i (h j)"),
                     in0=centred[b][:],
-                    scalar=inverse[:, b : b + 1],
+                    scalar=z_inverse[:, b : b + 1],
                     in1=bias[:].rearrange("i h j -> i (h j)"),
                     op0=ALU.mult,
                     op1=ALU.add,
                 )
                 nc.sync.dma_start(out=out_0[b].rearrange("(h i) j -> i h j", h=HALVES), in_=result[:])
+                if b == 0:
+                    nc.sync.dma_start(out=out_1.rearrange("b (h n) -> (b h) n", h=HALVES), in_=o_sum_rows[:])
 
         with tc.manual_schedule():
             load(0)
@@ -343,8 +355,9 @@ def tile_selfprojection_pa_k_kernel(
                     load(run + 1)
                 if 1 <= run < RUNS:
                     load_wj(run)
-                if 3 <= run < 7:
-                    load_wj_scales(EARLY_PASSES, PASSES, run - 3)
+                if 4 <= run + 3 < PASSES // 2:
+                    batch, r = divmod(run + 3, 4)
+                    load_wj_scales(batch * EARLY_PASSES, (batch + 1) * EARLY_PASSES, r)
                 if run >= 1:
                     quantise(run - 1)
                 if run + 1 < RUNS:
@@ -357,7 +370,7 @@ def tile_selfprojection_pa_k_kernel(
             for target, source in end_inputs:
                 nc.sync.dma_start(out=target, in_=source)
             nc.gpsimd.tensor_scalar(
-                out=bias_row_plus_1[:], in0=bias_row[:], scalar1=1.0, scalar2=1.0, op0=ALU.add, op1=ALU.mult
+                out=c_bias_plus_1[:], in0=c_bias[:], scalar1=1.0, scalar2=1.0, op0=ALU.add, op1=ALU.mult
             )
 
             finish()

@@ -29,7 +29,7 @@ RUNS = CHUNKS * BATCH
 RUN_LIST = [divmod(run, BATCH) for run in range(RUNS)]
 BANK_COLS = 256
 X_BUFS = 8
-EARLY_PASSES = 8
+SCALE_PASSES = 4
 
 FLOPS = 2 * BATCH * M * K * N + 2 * BATCH * N * M * N
 
@@ -188,7 +188,6 @@ def tile_selfprojection_pa_k_kernel(
 
         y_t, y_grouped, y_coded, z, centred = [{} for i in range(5)]
         c_cols = tail.tile([P, BATCH, HALVES], F32, name="c_cols")
-        z_mv = tail.tile([P, 2, BATCH], F32, name="z_mv")
 
         def copy_y_out(b):
             for h in range(HALVES):
@@ -243,11 +242,6 @@ def tile_selfprojection_pa_k_kernel(
                     stop=True,
                 )
 
-        def z_statistics(b):
-            z_stats = tail.tile([P, 6], F32, name="z_stats%d" % b)
-            nc.vector.bn_stats(out=z_stats[:], in_=z[b][:].rearrange("i h j -> i (h j)"))
-            nc.vector.bn_aggr(out=z_mv[:, :, b], in_=z_stats[:])
-
         def sum_of_halves(columns, name):
             total = banks.tile([P, BATCH], F32, tag="bank", name=name)
             for h in range(HALVES):
@@ -282,35 +276,53 @@ def tile_selfprojection_pa_k_kernel(
             for b in range(BATCH):
                 quantise_y(b)
                 multiply_y(b)
+            c_squares = sum_of_halves(c_square, "c_squares")
             c_spread = tail.tile([P, BATCH], F32, name="c_spread")
+            z_rows = [z[b][:].rearrange("i h j -> i (h j)") for b in range(BATCH)]
+            in_partition = HALVES * N
+            z_mean_var = tail.tile([P, 2, BATCH], F32, name="z_mean_var")
+            spare = tail.tile([P, in_partition], BF16, name="spare")
+            z_sum = tail.tile([P, 1], F32, name="z_sum")
+            nc.scalar.activation(out=spare[:], in_=z_rows[0], func=ACT.Copy, accum_out=z_sum[:])
+            minus_own = tail.tile([P, 1], F32, name="minus_own")
+            nc.scalar.mul(out=minus_own[:], in_=z_sum[:], mul=-1.0 / in_partition)
+            nc.scalar.mul(out=z_mean_var[:, 0, 0:1], in_=z_sum[:], mul=1.0 / in_partition)
+            z_square = tail.tile([P, 1], F32, name="z_square")
             nc.scalar.activation(
-                out=c_spread[:],
-                in_=sum_of_halves(c_square, "c_squares")[:],
-                func=ACT.Sqrt,
-                scale=1.0 / HALVES * N / (N - 1.0),
+                out=spare[:], in_=z_rows[0], func=ACT.Square, bias=minus_own[:], accum_out=z_square[:]
             )
-            for b in range(BATCH):
-                z_statistics(b)
+            z_stats = tail.tile([P, 6], F32, name="z_stats")
+            nc.vector.bn_stats(out=z_stats[:], in_=z_rows[1])
+            nc.vector.bn_aggr(out=z_mean_var[:, :, 1], in_=z_stats[:])
             means = banks.tile([P, 2, BATCH], F32, tag="bank", name="means")
-            nc.tensor.matmul(out=means[:, 0, :], lhsT=averager[:], rhs=z_mv[:, 0, :], start=True, stop=True)
+            nc.tensor.matmul(out=means[:, 0, :], lhsT=averager[:], rhs=z_mean_var[:, 0, :], start=True, stop=True)
+            distance = tail.tile([P, BATCH], F32, name="distance")
+            nc.vector.tensor_sub(out=distance[:], in0=z_mean_var[:, 0, :], in1=means[:, 0, :])
+            part_var = tail.tile([P, BATCH], F32, name="part_var")
+            nc.vector.tensor_mul(out=part_var[:], in0=distance[:], in1=distance[:])
+            nc.vector.scalar_tensor_tensor(
+                out=part_var[:, 0:1],
+                in0=z_square[:],
+                scalar=1.0 / in_partition,
+                in1=part_var[:, 0:1],
+                op0=ALU.mult,
+                op1=ALU.add,
+            )
+            nc.vector.tensor_add(out=part_var[:, 1:2], in0=part_var[:, 1:2], in1=z_mean_var[:, 1, 1:2])
+            nc.scalar.activation(
+                out=c_spread[:], in_=c_squares[:], func=ACT.Sqrt, scale=1.0 / HALVES * N / (N - 1.0)
+            )
+            z_mean = tail.tile([P, BATCH], F32, name="z_mean")
+            nc.scalar.copy(out=z_mean[:], in_=means[:, 0, :])
+            nc.tensor.matmul(out=means[:, 1, :], lhsT=averager[:], rhs=part_var[:], start=True, stop=True)
+            z_spread = tail.tile([P, BATCH], F32, name="z_spread")
+            nc.scalar.activation(out=z_spread[:], in_=means[:, 1, :], func=ACT.Sqrt, scale=N * N / (N * N - 1.0))
             c_inverse = inverse_of(c_spread, "c_inverse")
             nc.gpsimd.tensor_tensor(
                 out=c_wide[:, 0 : BATCH * HALVES].rearrange("n (b h) -> n b h", h=HALVES),
                 in0=c_distance[:],
                 in1=c_inverse[:].unsqueeze(2).to_broadcast([P, BATCH, HALVES]),
                 op=ALU.mult,
-            )
-            distance = tail.tile([P, BATCH], F32, name="distance")
-            nc.vector.tensor_sub(out=distance[:], in0=z_mv[:, 0, :], in1=means[:, 0, :])
-            part_var = tail.tile([P, BATCH], F32, name="part_var")
-            nc.vector.tensor_mul(out=part_var[:], in0=distance[:], in1=distance[:])
-            nc.vector.tensor_add(out=part_var[:], in0=part_var[:], in1=z_mv[:, 1, :])
-            z_mean = tail.tile([P, BATCH], F32, name="z_mean")
-            nc.scalar.copy(out=z_mean[:], in_=means[:, 0, :])
-            nc.tensor.matmul(out=means[:, 1, :], lhsT=averager[:], rhs=part_var[:], start=True, stop=True)
-            z_spread = tail.tile([P, BATCH], F32, name="z_spread")
-            nc.scalar.activation(
-                out=z_spread[:], in_=means[:, 1, :], func=ACT.Sqrt, scale=N * N / (N * N - 1.0)
             )
             c_bank = banks.tile([P, P], F32, tag="bank", name="c_bank")
             nc.tensor.transpose(out=c_bank[:], in_=c_wide[:], identity=ident[:])
@@ -322,7 +334,7 @@ def tile_selfprojection_pa_k_kernel(
                 centred[b] = tail.tile([P, HALVES * N], F32, name="centred%d" % b)
                 nc.vector.scalar_tensor_tensor(
                     out=centred[b][:],
-                    in0=z[b][:].rearrange("i h j -> i (h j)"),
+                    in0=z_rows[b],
                     scalar=z_mean[:, b : b + 1],
                     in1=gain[:].rearrange("i h j -> i (h j)"),
                     op0=ALU.subtract,
@@ -330,34 +342,35 @@ def tile_selfprojection_pa_k_kernel(
                 )
             z_inverse = inverse_of(z_spread, "z_inverse")
             for b in range(BATCH):
-                result = tail.tile([P, HALVES, N], F32, name="result%d" % b)
-                nc.vector.scalar_tensor_tensor(
-                    out=result[:].rearrange("i h j -> i (h j)"),
-                    in0=centred[b][:],
-                    scalar=z_inverse[:, b : b + 1],
-                    in1=bias[:].rearrange("i h j -> i (h j)"),
-                    op0=ALU.mult,
-                    op1=ALU.add,
-                )
-                nc.sync.dma_start(out=out_0[b].rearrange("(h i) j -> i h j", h=HALVES), in_=result[:])
-                if b == 0:
-                    nc.sync.dma_start(out=out_1.rearrange("b (h n) -> (b h) n", h=HALVES), in_=o_sum_rows[:])
+                for h in range(HALVES):
+                    result = tail.tile([P, N], F32, name="result%d%d" % (b, h))
+                    nc.vector.scalar_tensor_tensor(
+                        out=result[:],
+                        in0=centred[b][:, h * N : (h + 1) * N],
+                        scalar=z_inverse[:, b : b + 1],
+                        in1=bias[:, h, :],
+                        op0=ALU.mult,
+                        op1=ALU.add,
+                    )
+                    nc.sync.dma_start(out=out_0[b, h * P : (h + 1) * P, :], in_=result[:])
+                if b == 1:
+                    nc.scalar.dma_start(out=out_1.rearrange("b (h n) -> (b h) n", h=HALVES), in_=o_sum_rows[:])
 
         with tc.manual_schedule():
             load(0)
             load(1)
             load_wj(0)
             for r in range(4):
-                load_wj_scales(0, EARLY_PASSES, r)
+                load_wj_scales(0, SCALE_PASSES, r)
             sort_words(0)
             for run in range(RUNS + 1):
                 if 1 < run + 1 < RUNS:
                     load(run + 1)
                 if 1 <= run < RUNS:
                     load_wj(run)
-                if 4 <= run + 3 < PASSES // 2:
-                    batch, r = divmod(run + 3, 4)
-                    load_wj_scales(batch * EARLY_PASSES, (batch + 1) * EARLY_PASSES, r)
+                batch, r = divmod(run + 4, 4)
+                if batch < PASSES // SCALE_PASSES:
+                    load_wj_scales(batch * SCALE_PASSES, (batch + 1) * SCALE_PASSES, r)
                 if run >= 1:
                     quantise(run - 1)
                 if run + 1 < RUNS:

@@ -58,12 +58,12 @@ def tile_selfprojection_pa_k_kernel(
         sums = ctx.enter_context(tc.psum_pool(name="sums", bufs=1))
         banks = ctx.enter_context(tc.psum_pool(name="banks", bufs=4))
 
-        wj_scales = const.tile([P, PASSES, N], U8, align_bytes=64)
+        wj_scales = const.tile([P, PASSES, N], U8, align_bytes=256)
         nc.vector.memset(wj_scales[:].bitcast(I32), 0)
-        wi_scales = const.tile([P, N], U8, align_bytes=64)
+        wi_scales = const.tile([P, N], U8, align_bytes=256)
         nc.vector.memset(wi_scales[:].bitcast(I32), 0)
 
-        ident = const.tile([P, P], F32)
+        ident = const.tile([P, P], F32, align_bytes=256)
         make_identity(nc, ident[:])
         averager = const.tile([P, P], F32)
         nc.vector.memset(averager[:], 1.0 / P)
@@ -89,7 +89,7 @@ def tile_selfprojection_pa_k_kernel(
 
         def load(run):
             chunk, b = divmod(run, BATCH)
-            xs = x_pool.tile([P, ROW_TILES, RUN_K], BF16, name="xs")
+            xs = x_pool.tile([P, ROW_TILES, RUN_K], BF16, name="xs", align_bytes=256)
             nc.sync.dma_start(
                 out=xs[:],
                 in_=x[b, :, chunk * RUN_K : (chunk + 1) * RUN_K].rearrange("(r t) k -> r t k", t=ROW_TILES),
@@ -99,7 +99,7 @@ def tile_selfprojection_pa_k_kernel(
         def load_wj(run):
             chunk, b = RUN_LIST[run]
             if b == 0:
-                wj = w_pool.tile([P, RUN_PASSES, N], U32, align_bytes=64)
+                wj = w_pool.tile([P, RUN_PASSES, N], U32, align_bytes=256)
                 nc.sync.dma_start(
                     out=wj[:].bitcast(I32),
                     in_=wj_words[chunk * RUN_PASSES : (chunk + 1) * RUN_PASSES].rearrange("g p n -> p g n"),
@@ -108,7 +108,7 @@ def tile_selfprojection_pa_k_kernel(
 
         def sort_words(run):
             xs_words = x_tiles[run][:].bitcast(F32)
-            planes = work.tile([P, RUN_PASSES, ROW_TILES, 2, P], F32)
+            planes = work.tile([P, RUN_PASSES, ROW_TILES, 2, P], F32, align_bytes=256)
             for g in range(RUN_PASSES):
                 nc.vector.tensor_copy(
                     out=planes[:, g],
@@ -118,7 +118,7 @@ def tile_selfprojection_pa_k_kernel(
 
         def transpose(run):
             planes = sorted_tiles[run]
-            grouped = work.tile([P, RUN_PASSES, M, PACK], BF16, align_bytes=64)
+            grouped = work.tile([P, RUN_PASSES, M, PACK], BF16, align_bytes=256)
             grouped_words = grouped[:].bitcast(F32)
             for g in range(RUN_PASSES):
                 for c in range(M // BANK_COLS):
@@ -139,8 +139,8 @@ def tile_selfprojection_pa_k_kernel(
 
         def quantise(run):
             grouped = grouped_tiles[run]
-            codes = work.tile([P, RUN_PASSES, M], U32, align_bytes=64)
-            scales = work.tile([P, RUN_PASSES, M], U8, align_bytes=64)
+            codes = work.tile([P, RUN_PASSES, M], U32, align_bytes=256)
+            scales = work.tile([P, RUN_PASSES, M], U8, align_bytes=256)
             for g in range(RUN_PASSES):
                 nc.vector.quantize_mx(
                     out=codes[:, g, :].bitcast(FP8X4),
@@ -165,7 +165,7 @@ def tile_selfprojection_pa_k_kernel(
                         stop=(k_pass == PASSES - 1),
                     )
 
-        wi = const.tile([P, N], U32, name="wi", align_bytes=64)
+        wi = const.tile([P, N], U32, name="wi", align_bytes=256)
         gain = const.tile([P, HALVES, N], BF16, name="gain")
         bias = const.tile([P, HALVES, N], BF16, name="bias")
         c_gain = const.tile([BATCH * HALVES, P], BF16, name="c_gain")
@@ -208,7 +208,7 @@ def tile_selfprojection_pa_k_kernel(
                     )
 
         def turn_y(b):
-            y_grouped[b] = tail.tile([P, N, PACK], BF16, name="y_grouped%d" % b, align_bytes=64)
+            y_grouped[b] = tail.tile([P, N, PACK], BF16, name="y_grouped%d" % b, align_bytes=256)
             y_words = y_grouped[b][:].bitcast(F32)
             for h in range(HALVES):
                 y_bank = sums.tile([P, 2, P], F32, tag="sum%d%d" % (b, h), name="y_bank%d%d" % (b, h))
@@ -219,8 +219,8 @@ def tile_selfprojection_pa_k_kernel(
                 copy_out(out=y_words[:, h * P : (h + 1) * P, :], in_=y_bank[:].rearrange("r u n -> r n u"))
 
         def quantise_y(b):
-            y_codes = tail.tile([P, N], U32, name="y_codes%d" % b, align_bytes=64)
-            y_scales = tail.tile([P, N], U8, name="y_scales%d" % b, align_bytes=64)
+            y_codes = tail.tile([P, N], U32, name="y_codes%d" % b, align_bytes=256)
+            y_scales = tail.tile([P, N], U8, name="y_scales%d" % b, align_bytes=256)
             nc.vector.quantize_mx(
                 out=y_codes[:].bitcast(FP8X4),
                 scales=y_scales[:],

from contextlib import ExitStack

import concourse.mybir as mybir
from concourse.masks import make_identity

BF16 = mybir.dt.bfloat16
F32 = mybir.dt.float32
I32 = mybir.dt.int32
U32 = mybir.dt.uint32
U8 = mybir.dt.uint8
FP8X4 = mybir.dt.float8_e4m3fn_x4
ALU = mybir.AluOpType
ACT = mybir.ActivationFunctionType

P = 128
PACK = 4
K_PASS = P * PACK
BATCH, M, K, N = 2, 512, 16384, 256
EPS = 1e-05

PASSES = K // K_PASS
ROW_TILES = M // P
HALVES = N // P
WORDS = K_PASS // 2
RUN_PASSES = 2
RUN_K = RUN_PASSES * K_PASS
CHUNKS = PASSES // RUN_PASSES
RUNS = CHUNKS * BATCH
RUN_LIST = [divmod(run, BATCH) for run in range(RUNS)]
BANK_COLS = 256
X_BUFS = 8
SCALE_PASSES = 4

FLOPS = 2 * BATCH * M * K * N + 2 * BATCH * N * M * N


def tile_selfprojection_pa_k_kernel(
    tc,
    x,
    original_xj_y_words,
    original_xj_y_scales,
    original_xi_y_words,
    original_xi_y_scales,
    gamma_o_sum,
    gamma_o,
    beta_o_sum,
    beta_o,
    out_0,
    out_1,
):
    nc = tc.nc
    with ExitStack() as ctx:
        const = ctx.enter_context(tc.tile_pool(name="const", bufs=1))
        x_pool = ctx.enter_context(tc.tile_pool(name="x_pool", bufs=X_BUFS))
        w_pool = ctx.enter_context(tc.tile_pool(name="w_pool", bufs=CHUNKS))
        work = ctx.enter_context(tc.tile_pool(name="work", bufs=3))
        tail = ctx.enter_context(tc.tile_pool(name="tail", bufs=1))
        sums = ctx.enter_context(tc.psum_pool(name="sums", bufs=1))
        banks = ctx.enter_context(tc.psum_pool(name="banks", bufs=4))

        wj_scales = const.tile([P, PASSES, N], U8, align_bytes=256)
        nc.vector.memset(wj_scales[:].bitcast(I32), 0)
        wi_scales = const.tile([P, N], U8, align_bytes=256)
        nc.vector.memset(wi_scales[:].bitcast(I32), 0)

        ident = const.tile([P, P], F32, align_bytes=256)
        make_identity(nc, ident[:])
        averager = const.tile([P, P], F32)
        nc.vector.memset(averager[:], 1.0 / P)
        warm = const.tile([P, 1], F32)
        nc.vector.memset(warm[:], 1.0)
        nc.scalar.sqrt(out=warm[:], in_=warm[:])

        wj_words = original_xj_y_words.rearrange("g p n t -> g p (n t)").bitcast(I32)
        x_tiles = {}
        w_tiles = {}
        sorted_tiles = {}
        grouped_tiles = {}
        code_tiles = {}

        y_t_sums = {}
        for b in range(BATCH):
            for h in range(HALVES):
                y_t_sums[b, h] = sums.tile([P, M], F32, name="sum%d%d" % (b, h))

        def load_wj_scales(first, last, r):
            rows = original_xj_y_scales[first:last].bitcast(I32).rearrange("g (q r) n -> r q g n", r=4)
            nc.sync.dma_start(out=wj_scales[r:P:32, first:last, :].bitcast(I32), in_=rows[r])

        def load(run):
            chunk, b = divmod(run, BATCH)
            xs = x_pool.tile([P, ROW_TILES, RUN_K], BF16, name="xs", align_bytes=256)
            nc.sync.dma_start(
                out=xs[:],
                in_=x[b, :, chunk * RUN_K : (chunk + 1) * RUN_K].rearrange("(r t) k -> r t k", t=ROW_TILES),
            )
            x_tiles[run] = xs

        def load_wj(run):
            chunk, b = RUN_LIST[run]
            if b == 0:
                wj = w_pool.tile([P, RUN_PASSES, N], U32, align_bytes=256)
                nc.sync.dma_start(
                    out=wj[:].bitcast(I32),
                    in_=wj_words[chunk * RUN_PASSES : (chunk + 1) * RUN_PASSES].rearrange("g p n -> p g n"),
                )
                w_tiles[chunk] = wj

        def sort_words(run):
            xs_words = x_tiles[run][:].bitcast(F32)
            planes = work.tile([P, RUN_PASSES, ROW_TILES, 2, P], F32, align_bytes=256)
            for g in range(RUN_PASSES):
                nc.vector.tensor_copy(
                    out=planes[:, g],
                    in_=xs_words[:, :, g * WORDS : (g + 1) * WORDS].rearrange("r t (j u) -> r t u j", u=2),
                )
            sorted_tiles[run] = planes

        def transpose(run):
            planes = sorted_tiles[run]
            grouped = work.tile([P, RUN_PASSES, M, PACK], BF16, align_bytes=256)
            grouped_words = grouped[:].bitcast(F32)
            for g in range(RUN_PASSES):
                for c in range(M // BANK_COLS):
                    bank = banks.tile([P, 2, BANK_COLS], F32)
                    for i in range(BANK_COLS // P):
                        for u in range(2):
                            nc.tensor.transpose(
                                out=bank[:, u, i * P : (i + 1) * P],
                                in_=planes[:, g, c * (BANK_COLS // P) + i, u, :],
                                identity=ident[:],
                            )
                    copy_out = nc.vector.tensor_copy if (run, g, c) == (RUNS - 1, 1, 0) else nc.scalar.copy
                    copy_out(
                        out=grouped_words[:, g, c * BANK_COLS : (c + 1) * BANK_COLS, :],
                        in_=bank[:].rearrange("p u m -> p m u"),
                    )
            grouped_tiles[run] = grouped

        def quantise(run):
            grouped = grouped_tiles[run]
            codes = work.tile([P, RUN_PASSES, M], U32, align_bytes=256)
            scales = work.tile([P, RUN_PASSES, M], U8, align_bytes=256)
            for g in range(RUN_PASSES):
                nc.vector.quantize_mx(
                    out=codes[:, g, :].bitcast(FP8X4),
                    scales=scales[:, g, :],
                    in_=grouped[:, g].rearrange("p m t -> p (m t)"),
                )
            code_tiles[run] = (codes, scales)

        def multiply(run):
            chunk, b = RUN_LIST[run]
            codes, scales = code_tiles[run]
            for g in range(RUN_PASSES):
                k_pass = chunk * RUN_PASSES + g
                for h in range(HALVES):
                    nc.tensor.matmul_mx(
                        out=y_t_sums[b, h][:],
                        lhsT=w_tiles[chunk][:, g, h * P : (h + 1) * P].bitcast(FP8X4),
                        lhsT_scale=wj_scales[:, k_pass, h * P : (h + 1) * P],
                        rhs=codes[:, g, :].bitcast(FP8X4),
                        rhs_scale=scales[:, g, :],
                        start=(k_pass == 0),
                        stop=(k_pass == PASSES - 1),
                    )

        wi = const.tile([P, N], U32, name="wi", align_bytes=256)
        gain = const.tile([P, HALVES, N], BF16, name="gain")
        bias = const.tile([P, HALVES, N], BF16, name="bias")
        c_gain = const.tile([BATCH * HALVES, P], BF16, name="c_gain")
        c_bias = const.tile([BATCH * HALVES, P], BF16, name="c_bias")
        c_bias_plus_1 = const.tile([BATCH * HALVES, P], F32, name="c_bias_plus_1")
        c_wide = const.tile([P, P], F32, name="c_wide")
        nc.vector.memset(c_wide[:], 0.0)

        wi_scale_rows = original_xi_y_scales.bitcast(I32).rearrange("g (q r) n -> r (g q) n", r=4)
        end_inputs = [
            (wi[:].bitcast(I32), original_xi_y_words.rearrange("g p n t -> (g p) (n t)").bitcast(I32)),
        ]
        end_inputs.extend([(wi_scales[r:P:32].bitcast(I32), wi_scale_rows[r]) for r in range(4)])
        end_inputs.append((gain[:], gamma_o.rearrange("(h i) j -> i h j", h=HALVES)))
        end_inputs.append((bias[:], beta_o.rearrange("(h i) j -> i h j", h=HALVES)))
        for b in range(BATCH):
            rows = slice(b * HALVES, (b + 1) * HALVES)
            end_inputs.append((c_gain[rows, :], gamma_o_sum.rearrange("(h n) -> h n", h=HALVES)))
            end_inputs.append((c_bias[rows, :], beta_o_sum.rearrange("(h n) -> h n", h=HALVES)))

        y_t, y_grouped, y_coded, z, centred = [{} for i in range(5)]
        c_cols = tail.tile([P, BATCH, HALVES], F32, name="c_cols")

        def copy_y_out(b):
            for h in range(HALVES):
                y_t[b, h] = tail.tile([P, 2, P, 2], BF16, name="y_t%d%d" % (b, h))
                y_rows = y_t_sums[b, h][:].rearrange("n (u e r) -> n u r e", u=2, e=2)
                c_col = c_cols[:, b, h : h + 1]
                if h == 0:
                    nc.scalar.activation(out=y_t[b, h][:], in_=y_rows, func=ACT.Copy, accum_out=c_col)
                else:
                    nc.vector.tensor_scalar(
                        out=y_t[b, h][:],
                        in0=y_rows,
                        scalar1=1.0,
                        scalar2=None,
                        op0=ALU.mult,
                        op1=ALU.add,
                        accum_out=c_col,
                    )

        def turn_y(b):
            y_grouped[b] = tail.tile([P, N, PACK], BF16, name="y_grouped%d" % b, align_bytes=256)
            y_words = y_grouped[b][:].bitcast(F32)
            for h in range(HALVES):
                y_bank = sums.tile([P, 2, P], F32, tag="sum%d%d" % (b, h), name="y_bank%d%d" % (b, h))
                columns = y_t[b, h][:].rearrange("n u r e -> n (u r e)").bitcast(F32)
                for u in range(2):
                    nc.tensor.transpose(out=y_bank[:, u, :], in_=columns[:, u * P : (u + 1) * P], identity=ident[:])
                copy_out = nc.scalar.copy if h == 0 else nc.vector.tensor_copy
                copy_out(out=y_words[:, h * P : (h + 1) * P, :], in_=y_bank[:].rearrange("r u n -> r n u"))

        def quantise_y(b):
            y_codes = tail.tile([P, N], U32, name="y_codes%d" % b, align_bytes=256)
            y_scales = tail.tile([P, N], U8, name="y_scales%d" % b, align_bytes=256)
            nc.vector.quantize_mx(
                out=y_codes[:].bitcast(FP8X4),
                scales=y_scales[:],
                in_=y_grouped[b][:].rearrange("r j t -> r (j t)"),
            )
            y_coded[b] = (y_codes, y_scales)

        def multiply_y(b):
            y_codes, y_scales = y_coded[b]
            z[b] = sums.tile([P, HALVES, N], F32, tag="sum%d0" % b, name="z%d" % b)
            for h in range(HALVES):
                nc.tensor.matmul_mx(
                    out=z[b][:, h, :],
                    lhsT=wi[:, h * P : (h + 1) * P].bitcast(FP8X4),
                    lhsT_scale=wi_scales[:, h * P : (h + 1) * P],
                    rhs=y_codes[:].bitcast(FP8X4),
                    rhs_scale=y_scales[:],
                    start=True,
                    stop=True,
                )

        def sum_of_halves(columns, name):
            total = banks.tile([P, BATCH], F32, tag="bank", name=name)
            for h in range(HALVES):
                nc.tensor.matmul(
                    out=total[:], lhsT=averager[:], rhs=columns[:, :, h], start=(h == 0), stop=(h == HALVES - 1)
                )
            return total

        def inverse_of(spread, name):
            nc.vector.tensor_scalar_add(out=spread[:], in0=spread[:], scalar1=EPS)
            inverse = tail.tile([P, BATCH], F32, name=name)
            nc.vector.reciprocal(out=inverse[:], in_=spread[:])
            return inverse

        def finish():
            for b in range(BATCH):
                copy_y_out(b)
            for b in range(BATCH):
                turn_y(b)
            c_total = sum_of_halves(c_cols, "c_total")
            c_mean = tail.tile([P, BATCH], F32, name="c_mean")
            nc.scalar.mul(out=c_mean[:], in_=c_total[:], mul=1.0 / HALVES)
            c_distance = tail.tile([P, BATCH, HALVES], F32, name="c_distance")
            nc.gpsimd.tensor_tensor(
                out=c_distance[:],
                in0=c_cols[:],
                in1=c_mean[:].unsqueeze(2).to_broadcast([P, BATCH, HALVES]),
                op=ALU.subtract,
            )
            c_square = tail.tile([P, BATCH, HALVES], F32, name="c_square")
            nc.gpsimd.tensor_tensor(out=c_square[:], in0=c_distance[:], in1=c_distance[:], op=ALU.mult)
            for b in range(BATCH):
                quantise_y(b)
                multiply_y(b)
            c_squares = sum_of_halves(c_square, "c_squares")
            c_spread = tail.tile([P, BATCH], F32, name="c_spread")
            z_rows = [z[b][:].rearrange("i h j -> i (h j)") for b in range(BATCH)]
            in_partition = HALVES * N
            z_mean_var = tail.tile([P, 2, BATCH], F32, name="z_mean_var")
            spare = tail.tile([P, in_partition], BF16, name="spare")
            z_sum = tail.tile([P, 1], F32, name="z_sum")
            nc.scalar.activation(out=spare[:], in_=z_rows[0], func=ACT.Copy, accum_out=z_sum[:])
            minus_own = tail.tile([P, 1], F32, name="minus_own")
            nc.scalar.mul(out=minus_own[:], in_=z_sum[:], mul=-1.0 / in_partition)
            nc.scalar.mul(out=z_mean_var[:, 0, 0:1], in_=z_sum[:], mul=1.0 / in_partition)
            z_square = tail.tile([P, 1], F32, name="z_square")
            nc.scalar.activation(
                out=spare[:], in_=z_rows[0], func=ACT.Square, bias=minus_own[:], accum_out=z_square[:]
            )
            z_stats = tail.tile([P, 6], F32, name="z_stats")
            nc.vector.bn_stats(out=z_stats[:], in_=z_rows[1])
            nc.vector.bn_aggr(out=z_mean_var[:, :, 1], in_=z_stats[:])
            means = banks.tile([P, 2, BATCH], F32, tag="bank", name="means")
            nc.tensor.matmul(out=means[:, 0, :], lhsT=averager[:], rhs=z_mean_var[:, 0, :], start=True, stop=True)
            distance = tail.tile([P, BATCH], F32, name="distance")
            nc.vector.tensor_sub(out=distance[:], in0=z_mean_var[:, 0, :], in1=means[:, 0, :])
            part_var = tail.tile([P, BATCH], F32, name="part_var")
            nc.vector.tensor_mul(out=part_var[:], in0=distance[:], in1=distance[:])
            nc.vector.scalar_tensor_tensor(
                out=part_var[:, 0:1],
                in0=z_square[:],
                scalar=1.0 / in_partition,
                in1=part_var[:, 0:1],
                op0=ALU.mult,
                op1=ALU.add,
            )
            nc.vector.tensor_add(out=part_var[:, 1:2], in0=part_var[:, 1:2], in1=z_mean_var[:, 1, 1:2])
            nc.scalar.activation(
                out=c_spread[:], in_=c_squares[:], func=ACT.Sqrt, scale=1.0 / HALVES * N / (N - 1.0)
            )
            z_mean = tail.tile([P, BATCH], F32, name="z_mean")
            nc.scalar.copy(out=z_mean[:], in_=means[:, 0, :])
            nc.tensor.matmul(out=means[:, 1, :], lhsT=averager[:], rhs=part_var[:], start=True, stop=True)
            z_spread = tail.tile([P, BATCH], F32, name="z_spread")
            nc.scalar.activation(out=z_spread[:], in_=means[:, 1, :], func=ACT.Sqrt, scale=N * N / (N * N - 1.0))
            c_inverse = inverse_of(c_spread, "c_inverse")
            nc.gpsimd.tensor_tensor(
                out=c_wide[:, 0 : BATCH * HALVES].rearrange("n (b h) -> n b h", h=HALVES),
                in0=c_distance[:],
                in1=c_inverse[:].unsqueeze(2).to_broadcast([P, BATCH, HALVES]),
                op=ALU.mult,
            )
            c_bank = banks.tile([P, P], F32, tag="bank", name="c_bank")
            nc.tensor.transpose(out=c_bank[:], in_=c_wide[:], identity=ident[:])
            o_sum_rows = tail.tile([BATCH * HALVES, P], F32, name="o_sum_rows")
            nc.scalar.copy(out=o_sum_rows[:], in_=c_bank[0 : BATCH * HALVES, :])
            nc.gpsimd.tensor_tensor(out=o_sum_rows[:], in0=o_sum_rows[:], in1=c_gain[:], op=ALU.mult)
            nc.gpsimd.tensor_tensor(out=o_sum_rows[:], in0=o_sum_rows[:], in1=c_bias_plus_1[:], op=ALU.add)
            for b in range(BATCH):
                centred[b] = tail.tile([P, HALVES * N], F32, name="centred%d" % b)
                nc.vector.scalar_tensor_tensor(
                    out=centred[b][:],
                    in0=z_rows[b],
                    scalar=z_mean[:, b : b + 1],
                    in1=gain[:].rearrange("i h j -> i (h j)"),
                    op0=ALU.subtract,
                    op1=ALU.mult,
                )
            z_inverse = inverse_of(z_spread, "z_inverse")
            for b in range(BATCH):
                for h in range(HALVES):
                    result = tail.tile([P, N], F32, name="result%d%d" % (b, h))
                    nc.vector.scalar_tensor_tensor(
                        out=result[:],
                        in0=centred[b][:, h * N : (h + 1) * N],
                        scalar=z_inverse[:, b : b + 1],
                        in1=bias[:, h, :],
                        op0=ALU.mult,
                        op1=ALU.add,
                    )
                    nc.sync.dma_start(out=out_0[b, h * P : (h + 1) * P, :], in_=result[:])
                if b == 1:
                    nc.scalar.dma_start(out=out_1.rearrange("b (h n) -> (b h) n", h=HALVES), in_=o_sum_rows[:])

        with tc.manual_schedule():
            load(0)
            load(1)
            load_wj(0)
            for r in range(4):
                load_wj_scales(0, SCALE_PASSES, r)
            sort_words(0)
            for run in range(RUNS + 1):
                if 1 < run + 1 < RUNS:
                    load(run + 1)
                if 1 <= run < RUNS:
                    load_wj(run)
                batch, r = divmod(run + 4, 4)
                if batch < PASSES // SCALE_PASSES:
                    load_wj_scales(batch * SCALE_PASSES, (batch + 1) * SCALE_PASSES, r)
                if run >= 1:
                    quantise(run - 1)
                if run + 1 < RUNS:
                    sort_words(run + 1)
                if run < RUNS:
                    transpose(run)
                if run >= 1:
                    multiply(run - 1)

            for target, source in end_inputs:
                nc.sync.dma_start(out=target, in_=source)
            nc.gpsimd.tensor_scalar(
                out=c_bias_plus_1[:], in0=c_bias[:], scalar1=1.0, scalar2=1.0, op0=ALU.add, op1=ALU.mult
            )

            finish()
